import numpy as np
import ml_dtypes


def mxq(x, axis, fmt="e4m3"):
    dtype, down = {"e4m3": (ml_dtypes.float8_e4m3fn, 7), "e5m2": (ml_dtypes.float8_e5m2, 14)}[fmt]
    v = np.moveaxis(np.asarray(x, np.float32).astype(ml_dtypes.bfloat16).astype(np.float64), axis, -1)
    blocks = v.reshape(v.shape[:-1] + (-1, 32))
    amax = np.abs(blocks).max(-1, keepdims=True)
    byte = np.maximum(np.where(amax > 0, np.frexp(amax)[1] - 1 + 127, 0) - down, 1)
    scale = np.exp2(byte - 127.0)
    codes = (blocks / scale).astype(np.float32).astype(dtype).astype(np.float64)
    return np.moveaxis((codes * scale).reshape(v.shape), -1, axis)


WIDE = False


def mx_kscale(k):
    if not WIDE:
        return np.ones(k)
    levels = np.array([10, -10, 5, -5, 0])
    a = np.random.permutation(np.resize(levels, k // 512 * 4)).reshape(k // 512, 4)
    idx = np.arange(k)
    return np.exp2(a[idx // 512, idx % 128 // 32])


BF16 = ml_dtypes.bfloat16


def bf(x):
    return np.asarray(x, np.float32).astype(BF16)


def f64(x):
    return np.asarray(x).astype(np.float64)


E2M1 = np.array([0.0, 0.5, 1.0, 1.5, 2.0, 3.0, 4.0, 6.0, -0.0, -0.5, -1.0, -1.5, -2.0, -3.0, -4.0, -6.0])


def pack_weight(w, fmt):
    k, n = w.shape
    w = f64(bf(w)).reshape(k // 32, 32, n)
    amax = np.abs(w).max(1)
    if fmt == "e4m3":
        byte = np.frexp(amax)[1] - 1 + 127 - 7
    else:
        mant, ex = np.frexp(amax / 6.0)
        byte = np.where(mant > 0.5, ex, ex - 1) + 127
    byte = np.clip(np.where(amax > 0, byte, 1), 1, 254)
    scaled = (w * np.exp2(127.0 - byte)[:, None, :]).reshape(k, n).astype(np.float32)
    by_word = np.ascontiguousarray(scaled.reshape(k // 512, 128, 4, n).transpose(0, 1, 3, 2))
    if fmt == "e4m3":
        words = by_word.astype(ml_dtypes.float8_e4m3fn).view(np.uint8)
    else:
        c = by_word.astype(ml_dtypes.float4_e2m1fn).view(np.uint8) & 0xF
        words = c[..., 0::2] | (c[..., 1::2] << 4)
    return np.ascontiguousarray(words), np.ascontiguousarray(byte.astype(np.uint8).reshape(k // 512, 16, n))


def unpack_weight(words, scales, fmt):
    g, p, n, _ = words.shape
    if fmt == "e4m3":
        vals = np.ascontiguousarray(words).view(ml_dtypes.float8_e4m3fn).astype(np.float64)
    else:
        nib = np.empty((g, p, n, 4), np.uint8)
        nib[..., 0::2] = words & 0xF
        nib[..., 1::2] = words >> 4
        vals = E2M1[nib]
    vals = vals * np.repeat(np.exp2(scales.astype(np.float64) - 127.0), 8, axis=1)[..., None]
    return vals.transpose(0, 1, 3, 2).reshape(g * 512, n)


B, C, H, W, KS, CO = 2, 32, 163, 163, 4, 128
OH, OW = H - KS + 1, W - KS + 1
Q = C * KS * KS


def unfold_patches(x, k):
    oh, ow = x.shape[2] - k + 1, x.shape[3] - k + 1
    rows = []
    for di in range(k):
        cols = [x[:, :, di:di + oh, dj:dj + ow] for dj in range(k)]
        rows.append(np.stack(cols, axis=-1))
    return np.stack(rows, axis=-2)


def wide_factors():
    s = mx_kscale(Q)
    hi, lo = np.log2(s.max()), np.log2(s.min())
    n = np.arange(C)
    phi = np.exp2(np.round(hi + (lo - hi) * np.minimum(n, C - n) / (C / 2)))
    c, h, w = np.ogrid[:C, :H, :W]
    m, di, dj = np.ogrid[:C, :KS, :KS]
    return phi[(c * OH * OW + h * OW + w) % C], phi[(m + di * OW + dj) % C].reshape(Q)


def setup_inputs():
    fx, fw = wide_factors()
    x = bf(np.random.standard_normal((B, C, H, W)) * fx)
    words, scales = pack_weight(np.random.standard_normal((Q, CO)) / np.sqrt(Q) / fw[:, None], "e4m3")
    bias = bf(np.random.standard_normal(CO) * 0.3)
    return {"x": x, "weights_words": words, "weights_scales": scales, "bias": bias}


def reference(x, weights_words, weights_scales, bias):
    patches = unfold_patches(f64(x), KS)
    patches = patches.reshape(B, OH, OW, Q)
    out = (mxq(patches, 3, "e4m3") @ unpack_weight(weights_words, weights_scales, "e4m3")) + f64(bias)
    return np.transpose(out, (0, 3, 1, 2))

@@ -1,0 +1,171 @@
+from contextlib import ExitStack
+
+import concourse.mybir as mybir
+from concourse.masks import make_identity
+
+F32 = mybir.dt.float32
+BF16 = mybir.dt.bfloat16
+I32 = mybir.dt.int32
+U32 = mybir.dt.uint32
+U8 = mybir.dt.uint8
+FP8X4 = mybir.dt.float8_e4m3fn_x4
+
+P = 128
+BATCH = 2
+C_IN = 32
+SIDE_OUT = 160
+TAPS = 4
+C_OUT = 128
+K = C_IN * TAPS * TAPS
+FLOPS = 2 * BATCH * SIDE_OUT * SIDE_OUT * K * C_OUT
+
+STRIPS = SIDE_OUT // C_IN
+SEG_ROWS = 20
+SEG_COLS = SEG_ROWS * STRIPS
+SEGS_PER_IMAGE = SIDE_OUT // SEG_ROWS
+IMAGES_PER_SWEEP = P // SEGS_PER_IMAGE
+SWEEPS = BATCH * C_IN // IMAGES_PER_SWEEP
+ROWS_LOADED = SEG_ROWS + TAPS - 1
+
+WORDS_USED = SIDE_OUT // 2 + 1
+WORD_PITCH = 88
+WINDOW_WORDS = WORDS_USED * 2 * TAPS
+
+GROUP_ROWS = 4
+GROUPS = SEG_ROWS // GROUP_ROWS
+PASS_COLS = 4
+PASSES_PER_GROUP = GROUP_ROWS * STRIPS // PASS_COLS
+BANK_COLS = 2
+
+VECTOR_TAKES_EVERY = 4
+
+
+def load_weights(nc, const, weights_words, weights_scales):
+    w_codes = const.tile([P, 4 * C_OUT], U8, align_bytes=64)
+    nc.sync.dma_start(
+        out=w_codes[:].bitcast(I32),
+        in_=weights_words[0].rearrange("p n t -> p (n t)").bitcast(I32),
+    )
+    w_scales = const.tile([P, C_OUT], U8, align_bytes=64)
+    nc.vector.memset(w_scales[:].bitcast(I32), 0)
+    for quadrant in range(4):
+        nc.sync.dma_start(
+            out=w_scales[32 * quadrant : 32 * quadrant + 4, :].bitcast(I32),
+            in_=weights_scales[0, 4 * quadrant : 4 * quadrant + 4, :].bitcast(I32),
+        )
+    return w_codes, w_scales
+
+
+def bias_on_partitions(nc, const, acc_psum, identity, bias):
+    bias_row = const.tile([1, C_OUT], BF16)
+    nc.sync.dma_start(out=bias_row[:], in_=bias.unsqueeze(0))
+    bias_square = const.tile([P, C_OUT], F32)
+    nc.vector.memset(bias_square[:], 0.0)
+    nc.vector.tensor_copy(out=bias_square[0:1, :], in_=bias_row[:])
+    bias_turned = acc_psum.tile([P, PASS_COLS * P], F32, tag="acc")
+    nc.tensor.transpose(bias_turned[:, 0:P], bias_square[:], identity[:])
+    bias_column = const.tile([P, 1], F32)
+    nc.vector.tensor_copy(out=bias_column[:], in_=bias_turned[:, 0:1])
+    return bias_column
+
+
+def tile_conv2d_kernel(tc, x, weights_words, weights_scales, bias, out):
+    nc = tc.nc
+    with ExitStack() as ctx:
+        const = ctx.enter_context(tc.tile_pool(name="const", bufs=1))
+        image_pool = ctx.enter_context(tc.tile_pool(name="image", bufs=2))
+        window_pool = ctx.enter_context(tc.tile_pool(name="windows", bufs=3))
+        patch_pool = ctx.enter_context(tc.tile_pool(name="patches", bufs=4))
+        code_pool = ctx.enter_context(tc.tile_pool(name="codes", bufs=4))
+        result_pool = ctx.enter_context(tc.tile_pool(name="result", bufs=2))
+        turn_psum = ctx.enter_context(tc.psum_pool(name="turned", bufs=4))
+        acc_psum = ctx.enter_context(tc.psum_pool(name="acc", bufs=4))
+
+        identity = const.tile([P, P], F32)
+        make_identity(nc, identity[:])
+        w_codes, w_scales = load_weights(nc, const, weights_words, weights_scales)
+        bias_column = bias_on_partitions(nc, const, acc_psum, identity, bias)
+
+        banks_turned = 0
+        for sweep in range(SWEEPS):
+            batch, first_image = divmod(sweep * IMAGES_PER_SWEEP, C_IN)
+
+            image = image_pool.tile([P, 2, ROWS_LOADED, 2 * WORD_PITCH], BF16)
+            for shift in range(2):
+                for seg in range(SEGS_PER_IMAGE):
+                    nc.sync.dma_start(
+                        out=image[seg:P:SEGS_PER_IMAGE, shift, :, 0 : 2 * WORDS_USED],
+                        in_=x[
+                            batch,
+                            first_image : first_image + IMAGES_PER_SWEEP,
+                            seg * SEG_ROWS : seg * SEG_ROWS + ROWS_LOADED,
+                            shift : shift + 2 * WORDS_USED,
+                        ],
+                    )
+            image_words = image[:].bitcast(F32)
+
+            result = result_pool.tile([P, P, SEG_COLS], F32)
+            for group in range(GROUPS):
+                windows = window_pool.tile([P, GROUP_ROWS, WINDOW_WORDS], F32)
+                windows_by_tap = windows[:].rearrange("p r (w e d) -> p r w e d", e=2, d=TAPS)
+                for row in range(GROUP_ROWS):
+                    top = group * GROUP_ROWS + row
+                    for shift in range(2):
+                        nc.vector.tensor_copy(
+                            out=windows_by_tap[:, row, :, shift, :],
+                            in_=image_words[:, shift, top : top + TAPS, 0:WORDS_USED].rearrange("p d w -> p w d"),
+                        )
+
+                for step in range(PASSES_PER_GROUP):
+                    patches = patch_pool.tile([P, PASS_COLS, P, TAPS], BF16, align_bytes=64)
+                    patch_words = patches[:].bitcast(F32)
+                    for half in range(PASS_COLS // BANK_COLS):
+                        turned = turn_psum.tile([P, BANK_COLS, 2, P], F32)
+                        for slot in range(BANK_COLS):
+                            row, strip = divmod(step * PASS_COLS + half * BANK_COLS + slot, STRIPS)
+                            for pair in range(2):
+                                first_word = 2 * TAPS * (16 * strip + pair)
+                                nc.tensor.transpose(
+                                    turned[:, slot, pair, :],
+                                    windows[:, row, first_word : first_word + P],
+                                    identity[:],
+                                )
+                        copy_out = patch_words[:, half * BANK_COLS : (half + 1) * BANK_COLS, :, :]
+                        copy_in = turned[:].rearrange("p c u s -> p c s u")
+                        banks_turned += 1
+                        if banks_turned % VECTOR_TAKES_EVERY == 0:
+                            nc.vector.tensor_copy(out=copy_out, in_=copy_in)
+                        else:
+                            nc.scalar.copy(out=copy_out, in_=copy_in)
+
+                    a_codes = code_pool.tile([P, PASS_COLS * P], U32, align_bytes=64)
+                    a_scales = code_pool.tile([P, PASS_COLS * P], U8, align_bytes=64)
+                    nc.vector.quantize_mx(
+                        out=a_codes[:].bitcast(FP8X4),
+                        scales=a_scales[:],
+                        in_=patches[:].rearrange("p c s t -> p (c s t)"),
+                    )
+
+                    acc = acc_psum.tile([P, PASS_COLS * P], F32)
+                    nc.tensor.matmul_mx(
+                        out=acc[:],
+                        lhsT=w_codes[:].bitcast(FP8X4),
+                        lhsT_scale=w_scales[:],
+                        rhs=a_codes[:].bitcast(FP8X4),
+                        rhs_scale=a_scales[:],
+                        start=True,
+                        stop=True,
+                    )
+                    first_col = (group * PASSES_PER_GROUP + step) * PASS_COLS
+                    nc.scalar.activation(
+                        out=result[:, :, first_col : first_col + PASS_COLS],
+                        in_=acc[:].rearrange("o (c s) -> o s c", c=PASS_COLS),
+                        func=mybir.ActivationFunctionType.Identity,
+                        bias=bias_column[:, 0:1],
+                    )
+
+            first_r = first_image * SIDE_OUT * STRIPS
+            nc.sync.dma_start(
+                out=out[batch].rearrange("o u v -> o (u v)")[:, first_r : first_r + P * SEG_COLS],
+                in_=result[:].rearrange("o s c -> o (s c)"),
+            )

@@ -35,6 +35,7 @@ GROUP_ROWS = 4
 GROUPS = SEG_ROWS // GROUP_ROWS
 PASS_COLS = 4
 PASSES_PER_GROUP = GROUP_ROWS * STRIPS // PASS_COLS
+PASSES = SWEEPS * GROUPS * PASSES_PER_GROUP
 BANK_COLS = 2
 
 VECTOR_TAKES_EVERY = 4
@@ -58,7 +59,7 @@ def load_weights(nc, const, weights_words, weights_scales):
 
 def bias_on_partitions(nc, const, acc_psum, identity, bias):
     bias_row = const.tile([1, C_OUT], BF16)
-    nc.sync.dma_start(out=bias_row[:], in_=bias.unsqueeze(0))
+    nc.scalar.dma_start(out=bias_row[:], in_=bias.unsqueeze(0))
     bias_square = const.tile([P, C_OUT], F32)
     nc.vector.memset(bias_square[:], 0.0)
     nc.vector.tensor_copy(out=bias_square[0:1, :], in_=bias_row[:])
@@ -75,97 +76,146 @@ def tile_conv2d_kernel(tc, x, weights_words, weights_scales, bias, out):
         const = ctx.enter_context(tc.tile_pool(name="const", bufs=1))
         image_pool = ctx.enter_context(tc.tile_pool(name="image", bufs=2))
         window_pool = ctx.enter_context(tc.tile_pool(name="windows", bufs=3))
-        patch_pool = ctx.enter_context(tc.tile_pool(name="patches", bufs=4))
-        code_pool = ctx.enter_context(tc.tile_pool(name="codes", bufs=4))
+        patch_pool = ctx.enter_context(tc.tile_pool(name="patches", bufs=3))
+        code_pool = ctx.enter_context(tc.tile_pool(name="codes", bufs=3))
         result_pool = ctx.enter_context(tc.tile_pool(name="result", bufs=2))
         turn_psum = ctx.enter_context(tc.psum_pool(name="turned", bufs=4))
         acc_psum = ctx.enter_context(tc.psum_pool(name="acc", bufs=4))
+        ctx.enter_context(tc.manual_schedule())
 
-        identity = const.tile([P, P], F32)
-        make_identity(nc, identity[:])
-        w_codes, w_scales = load_weights(nc, const, weights_words, weights_scales)
-        bias_column = bias_on_partitions(nc, const, acc_psum, identity, bias)
+        image_of = {}
+        result_of = {}
+        windows_of = {}
+        turned_of = {}
+        patches_of = {}
+        codes_of = {}
+        acc_of = {}
 
-        banks_turned = 0
-        for sweep in range(SWEEPS):
+        def load_image_rows(sweep, row_from, row_to):
             batch, first_image = divmod(sweep * IMAGES_PER_SWEEP, C_IN)
-
-            image = image_pool.tile([P, 2, ROWS_LOADED, 2 * WORD_PITCH], BF16)
+            if row_from == 0:
+                image_of[sweep] = image_pool.tile([P, 2, ROWS_LOADED, 2 * WORD_PITCH], BF16, name="image")
+            image = image_of[sweep]
             for shift in range(2):
                 for seg in range(SEGS_PER_IMAGE):
                     nc.sync.dma_start(
-                        out=image[seg:P:SEGS_PER_IMAGE, shift, :, 0 : 2 * WORDS_USED],
+                        out=image[seg:P:SEGS_PER_IMAGE, shift, row_from:row_to, 0 : 2 * WORDS_USED],
                         in_=x[
                             batch,
                             first_image : first_image + IMAGES_PER_SWEEP,
-                            seg * SEG_ROWS : seg * SEG_ROWS + ROWS_LOADED,
+                            seg * SEG_ROWS + row_from : seg * SEG_ROWS + row_to,
                             shift : shift + 2 * WORDS_USED,
                         ],
                     )
-            image_words = image[:].bitcast(F32)
 
-            result = result_pool.tile([P, P, SEG_COLS], F32)
-            for group in range(GROUPS):
-                windows = window_pool.tile([P, GROUP_ROWS, WINDOW_WORDS], F32)
-                windows_by_tap = windows[:].rearrange("p r (w e d) -> p r w e d", e=2, d=TAPS)
-                for row in range(GROUP_ROWS):
-                    top = group * GROUP_ROWS + row
-                    for shift in range(2):
-                        nc.vector.tensor_copy(
-                            out=windows_by_tap[:, row, :, shift, :],
-                            in_=image_words[:, shift, top : top + TAPS, 0:WORDS_USED].rearrange("p d w -> p w d"),
+        def build_window_row(group, row):
+            sweep, group_in_sweep = divmod(group, GROUPS)
+            if row == 0:
+                windows_of[group] = window_pool.tile([P, GROUP_ROWS, WINDOW_WORDS], F32, name="windows")
+            windows_by_tap = windows_of[group][:].rearrange("p r (w e d) -> p r w e d", e=2, d=TAPS)
+            image_words = image_of[sweep][:].bitcast(F32)
+            top = group_in_sweep * GROUP_ROWS + row
+            for shift in range(2):
+                nc.vector.tensor_copy(
+                    out=windows_by_tap[:, row, :, shift, :],
+                    in_=image_words[:, shift, top : top + TAPS, 0:WORDS_USED].rearrange("p d w -> p w d"),
+                )
+
+        def turn(n):
+            group, step = divmod(n, PASSES_PER_GROUP)
+            windows = windows_of[group]
+            turned_of[n] = []
+            for half in range(PASS_COLS // BANK_COLS):
+                turned = turn_psum.tile([P, BANK_COLS, 2, P], F32, name="turned")
+                turned_of[n].append(turned)
+                for slot in range(BANK_COLS):
+                    row, strip = divmod(step * PASS_COLS + half * BANK_COLS + slot, STRIPS)
+                    for pair in range(2):
+                        first_word = 2 * TAPS * (16 * strip + pair)
+                        nc.tensor.transpose(
+                            turned[:, slot, pair, :],
+                            windows[:, row, first_word : first_word + P],
+                            identity[:],
                         )
 
-                for step in range(PASSES_PER_GROUP):
-                    patches = patch_pool.tile([P, PASS_COLS, P, TAPS], BF16, align_bytes=64)
-                    patch_words = patches[:].bitcast(F32)
-                    for half in range(PASS_COLS // BANK_COLS):
-                        turned = turn_psum.tile([P, BANK_COLS, 2, P], F32)
-                        for slot in range(BANK_COLS):
-                            row, strip = divmod(step * PASS_COLS + half * BANK_COLS + slot, STRIPS)
-                            for pair in range(2):
-                                first_word = 2 * TAPS * (16 * strip + pair)
-                                nc.tensor.transpose(
-                                    turned[:, slot, pair, :],
-                                    windows[:, row, first_word : first_word + P],
-                                    identity[:],
-                                )
-                        copy_out = patch_words[:, half * BANK_COLS : (half + 1) * BANK_COLS, :, :]
-                        copy_in = turned[:].rearrange("p c u s -> p c s u")
-                        banks_turned += 1
-                        if banks_turned % VECTOR_TAKES_EVERY == 0:
-                            nc.vector.tensor_copy(out=copy_out, in_=copy_in)
-                        else:
-                            nc.scalar.copy(out=copy_out, in_=copy_in)
+        def copy_out(n):
+            patches = patch_pool.tile([P, PASS_COLS, P, TAPS], BF16, align_bytes=64, name="patches")
+            patches_of[n] = patches
+            patch_words = patches[:].bitcast(F32)
+            for half in range(PASS_COLS // BANK_COLS):
+                copy_to = patch_words[:, half * BANK_COLS : (half + 1) * BANK_COLS, :, :]
+                copy_from = turned_of[n][half][:].rearrange("p c u s -> p c s u")
+                bank = n * (PASS_COLS // BANK_COLS) + half
+                if bank % VECTOR_TAKES_EVERY == VECTOR_TAKES_EVERY - 1:
+                    nc.vector.tensor_copy(out=copy_to, in_=copy_from)
+                else:
+                    nc.scalar.copy(out=copy_to, in_=copy_from)
 
-                    a_codes = code_pool.tile([P, PASS_COLS * P], U32, align_bytes=64)
-                    a_scales = code_pool.tile([P, PASS_COLS * P], U8, align_bytes=64)
-                    nc.vector.quantize_mx(
-                        out=a_codes[:].bitcast(FP8X4),
-                        scales=a_scales[:],
-                        in_=patches[:].rearrange("p c s t -> p (c s t)"),
-                    )
-
-                    acc = acc_psum.tile([P, PASS_COLS * P], F32)
-                    nc.tensor.matmul_mx(
-                        out=acc[:],
-                        lhsT=w_codes[:].bitcast(FP8X4),
-                        lhsT_scale=w_scales[:],
-                        rhs=a_codes[:].bitcast(FP8X4),
-                        rhs_scale=a_scales[:],
-                        start=True,
-                        stop=True,
-                    )
-                    first_col = (group * PASSES_PER_GROUP + step) * PASS_COLS
-                    nc.scalar.activation(
-                        out=result[:, :, first_col : first_col + PASS_COLS],
-                        in_=acc[:].rearrange("o (c s) -> o s c", c=PASS_COLS),
-                        func=mybir.ActivationFunctionType.Identity,
-                        bias=bias_column[:, 0:1],
-                    )
-
-            first_r = first_image * SIDE_OUT * STRIPS
-            nc.sync.dma_start(
-                out=out[batch].rearrange("o u v -> o (u v)")[:, first_r : first_r + P * SEG_COLS],
-                in_=result[:].rearrange("o s c -> o (s c)"),
+        def quantise(n):
+            a_codes = code_pool.tile([P, PASS_COLS * P], U32, align_bytes=64, name="a_codes")
+            a_scales = code_pool.tile([P, PASS_COLS * P], U8, align_bytes=64, name="a_scales")
+            codes_of[n] = (a_codes, a_scales)
+            nc.vector.quantize_mx(
+                out=a_codes[:].bitcast(FP8X4),
+                scales=a_scales[:],
+                in_=patches_of[n][:].rearrange("p c s t -> p (c s t)"),
             )
+
+        def multiply(n):
+            a_codes, a_scales = codes_of[n]
+            acc = acc_psum.tile([P, PASS_COLS * P], F32, name="acc")
+            acc_of[n] = acc
+            nc.tensor.matmul_mx(
+                out=acc[:],
+                lhsT=w_codes[:].bitcast(FP8X4),
+                lhsT_scale=w_scales[:],
+                rhs=a_codes[:].bitcast(FP8X4),
+                rhs_scale=a_scales[:],
+                start=True,
+                stop=True,
+            )
+
+        def finish(n):
+            sweep, pass_in_sweep = divmod(n, GROUPS * PASSES_PER_GROUP)
+            if pass_in_sweep == 0:
+                result_of[sweep] = result_pool.tile([P, P, SEG_COLS], F32, name="result")
+            result = result_of[sweep]
+            first_col = pass_in_sweep * PASS_COLS
+            nc.scalar.activation(
+                out=result[:, :, first_col : first_col + PASS_COLS],
+                in_=acc_of[n][:].rearrange("o (c s) -> o s c", c=PASS_COLS),
+                func=mybir.ActivationFunctionType.Identity,
+                bias=bias_column[:, 0:1],
+            )
+            if pass_in_sweep == GROUPS * PASSES_PER_GROUP - 1:
+                batch, first_image = divmod(sweep * IMAGES_PER_SWEEP, C_IN)
+                first_r = first_image * SIDE_OUT * STRIPS
+                nc.sync.dma_start(
+                    out=out[batch].rearrange("o u v -> o (u v)")[:, first_r : first_r + P * SEG_COLS],
+                    in_=result[:].rearrange("o s c -> o (s c)"),
+                )
+
+        load_image_rows(0, 0, GROUP_ROWS + TAPS - 1)
+        identity = const.tile([P, P], F32)
+        make_identity(nc, identity[:])
+        w_codes, w_scales = load_weights(nc, const, weights_words, weights_scales)
+        load_image_rows(0, GROUP_ROWS + TAPS - 1, ROWS_LOADED)
+        bias_column = bias_on_partitions(nc, const, acc_psum, identity, bias)
+        for row in range(GROUP_ROWS):
+            build_window_row(0, row)
+
+        for n in range(PASSES + 3):
+            group, step = divmod(n, PASSES_PER_GROUP)
+            if n < PASSES:
+                if n % (GROUPS * PASSES_PER_GROUP) == 0 and n // (GROUPS * PASSES_PER_GROUP) + 1 < SWEEPS:
+                    load_image_rows(n // (GROUPS * PASSES_PER_GROUP) + 1, 0, ROWS_LOADED)
+                turn(n)
+                copy_out(n)
+            if 0 <= n - 1 < PASSES:
+                quantise(n - 1)
+            if step < GROUP_ROWS and group + 1 < SWEEPS * GROUPS:
+                build_window_row(group + 1, step)
+            if 0 <= n - 2 < PASSES:
+                multiply(n - 2)
+            if 0 <= n - 3 < PASSES:
+                finish(n - 3)

@@ -32,13 +32,29 @@ WORD_PITCH = 88
 WINDOW_WORDS = WORDS_USED * 2 * TAPS
 
 GROUP_ROWS = 4
+GROUP_COLS = GROUP_ROWS * STRIPS
 GROUPS = SEG_ROWS // GROUP_ROWS
-PASS_COLS = 4
-PASSES_PER_GROUP = GROUP_ROWS * STRIPS // PASS_COLS
-PASSES = SWEEPS * GROUPS * PASSES_PER_GROUP
-BANK_COLS = 2
+ALL_GROUPS = SWEEPS * GROUPS
+COPIED_ROW = 1
+TURNED_ROWS = [row for row in range(GROUP_ROWS) if row != COPIED_ROW]
+TURNED_COLS = [col for col in range(GROUP_COLS) if col // STRIPS != COPIED_ROW]
 
-VECTOR_TAKES_EVERY = 4
+BANK_COLS = 2
+BANKS = (len(TURNED_COLS) + BANK_COLS - 1) // BANK_COLS
+
+PASS_COLS = 4
+PASSES_PER_GROUP = GROUP_COLS // PASS_COLS
+PASSES_PER_SWEEP = GROUPS * PASSES_PER_GROUP
+LATE_PASSES = [
+    step
+    for step in range(PASSES_PER_GROUP)
+    if step * PASS_COLS < (COPIED_ROW + 1) * STRIPS and (step + 1) * PASS_COLS > COPIED_ROW * STRIPS
+]
+EARLY_PASSES = [step for step in range(PASSES_PER_GROUP) if step not in LATE_PASSES]
+
+STORE_PARTS = 4
+
+VECTOR_TAKES_EVERY = 3
 
 
 def load_weights(nc, const, weights_words, weights_scales):
@@ -86,85 +102,98 @@ def tile_conv2d_kernel(tc, x, weights_words, weights_scales, bias, out):
         image_of = {}
         result_of = {}
         windows_of = {}
-        turned_of = {}
         patches_of = {}
+        turned_of = {}
         codes_of = {}
         acc_of = {}
 
-        def load_image_rows(sweep, row_from, row_to):
-            batch, first_image = divmod(sweep * IMAGES_PER_SWEEP, C_IN)
-            if row_from == 0:
-                image_of[sweep] = image_pool.tile([P, 2, ROWS_LOADED, 2 * WORD_PITCH], BF16, name="image")
-            image = image_of[sweep]
-            for shift in range(2):
-                for seg in range(SEGS_PER_IMAGE):
-                    nc.sync.dma_start(
-                        out=image[seg:P:SEGS_PER_IMAGE, shift, row_from:row_to, 0 : 2 * WORDS_USED],
-                        in_=x[
-                            batch,
-                            first_image : first_image + IMAGES_PER_SWEEP,
-                            seg * SEG_ROWS + row_from : seg * SEG_ROWS + row_to,
-                            shift : shift + 2 * WORDS_USED,
-                        ],
-                    )
+        def new_image(sweep):
+            image_of[sweep] = image_pool.tile([P, 2, ROWS_LOADED, 2 * WORD_PITCH], BF16, name="image")
 
-        def build_window_row(group, row):
+        def load_image_row(sweep, row, shift):
+            batch, first_image = divmod(sweep * IMAGES_PER_SWEEP, C_IN)
+            nc.sync.dma_start(
+                out=image_of[sweep][:, shift, row, 0 : 2 * WORDS_USED],
+                in_=x[
+                    batch,
+                    first_image : first_image + IMAGES_PER_SWEEP,
+                    row : row + (SEGS_PER_IMAGE - 1) * SEG_ROWS + 1 : SEG_ROWS,
+                    shift : shift + 2 * WORDS_USED,
+                ],
+            )
+
+        def load_image_segments(sweep, seg, shift):
+            batch, first_image = divmod(sweep * IMAGES_PER_SWEEP, C_IN)
+            nc.sync.dma_start(
+                out=image_of[sweep][seg:P:SEGS_PER_IMAGE, shift, :, 0 : 2 * WORDS_USED],
+                in_=x[
+                    batch,
+                    first_image : first_image + IMAGES_PER_SWEEP,
+                    seg * SEG_ROWS : seg * SEG_ROWS + ROWS_LOADED,
+                    shift : shift + 2 * WORDS_USED,
+                ],
+            )
+
+        def build_window(group, turned_row, shift):
             sweep, group_in_sweep = divmod(group, GROUPS)
-            if row == 0:
-                windows_of[group] = window_pool.tile([P, GROUP_ROWS, WINDOW_WORDS], F32, name="windows")
+            if turned_row == 0 and shift == 0:
+                windows_of[group] = window_pool.tile([P, len(TURNED_ROWS), WINDOW_WORDS], F32, name="windows")
             windows_by_tap = windows_of[group][:].rearrange("p r (w e d) -> p r w e d", e=2, d=TAPS)
             image_words = image_of[sweep][:].bitcast(F32)
-            top = group_in_sweep * GROUP_ROWS + row
-            for shift in range(2):
-                nc.vector.tensor_copy(
-                    out=windows_by_tap[:, row, :, shift, :],
-                    in_=image_words[:, shift, top : top + TAPS, 0:WORDS_USED].rearrange("p d w -> p w d"),
+            top = group_in_sweep * GROUP_ROWS + TURNED_ROWS[turned_row]
+            nc.vector.tensor_copy(
+                out=windows_by_tap[:, turned_row, :, shift, :],
+                in_=image_words[:, shift, top : top + TAPS, 0:WORDS_USED].rearrange("p d w -> p w d"),
+            )
+
+        def turn(group, bank):
+            turned = turn_psum.tile([P, BANK_COLS, 2, P], F32, name="turned")
+            turned_of[(group, bank)] = turned
+            for slot, col in enumerate(TURNED_COLS[bank * BANK_COLS : (bank + 1) * BANK_COLS]):
+                row, strip = divmod(col, STRIPS)
+                for pair in range(2):
+                    first_word = 2 * TAPS * (16 * strip + pair)
+                    nc.tensor.transpose(
+                        turned[:, slot, pair, :],
+                        windows_of[group][:, TURNED_ROWS.index(row), first_word : first_word + P],
+                        identity[:],
+                    )
+
+        def copy_out(group, bank):
+            if bank == 0:
+                patches_of[group] = patch_pool.tile([P, GROUP_COLS, P, TAPS], BF16, align_bytes=64, name="patches")
+            patch_words = patches_of[group][:].bitcast(F32)
+            cols = TURNED_COLS[bank * BANK_COLS : (bank + 1) * BANK_COLS]
+            copy_to = patch_words[:, cols[0] : cols[-1] + 1 : max(cols[-1] - cols[0], 1), :, :]
+            copy_from = turned_of[(group, bank)][:, 0 : len(cols), :, :].rearrange("p c u s -> p c s u")
+            if (group * BANKS + bank) % VECTOR_TAKES_EVERY == VECTOR_TAKES_EVERY - 1:
+                nc.vector.tensor_copy(out=copy_to, in_=copy_from)
+            else:
+                nc.scalar.copy(out=copy_to, in_=copy_from)
+
+        def copy_row(group, taps_to, taps_from, row_from):
+            patches = patches_of[group]
+            for tap_to, tap_from in zip(taps_to, taps_from):
+                nc.sync.dma_start(
+                    out=patches[tap_to:P:TAPS, COPIED_ROW * STRIPS : (COPIED_ROW + 1) * STRIPS, :, :],
+                    in_=patches[tap_from:P:TAPS, row_from * STRIPS : (row_from + 1) * STRIPS, :, :],
                 )
 
-        def turn(n):
-            group, step = divmod(n, PASSES_PER_GROUP)
-            windows = windows_of[group]
-            turned_of[n] = []
-            for half in range(PASS_COLS // BANK_COLS):
-                turned = turn_psum.tile([P, BANK_COLS, 2, P], F32, name="turned")
-                turned_of[n].append(turned)
-                for slot in range(BANK_COLS):
-                    row, strip = divmod(step * PASS_COLS + half * BANK_COLS + slot, STRIPS)
-                    for pair in range(2):
-                        first_word = 2 * TAPS * (16 * strip + pair)
-                        nc.tensor.transpose(
-                            turned[:, slot, pair, :],
-                            windows[:, row, first_word : first_word + P],
-                            identity[:],
-                        )
-
-        def copy_out(n):
-            patches = patch_pool.tile([P, PASS_COLS, P, TAPS], BF16, align_bytes=64, name="patches")
-            patches_of[n] = patches
-            patch_words = patches[:].bitcast(F32)
-            for half in range(PASS_COLS // BANK_COLS):
-                copy_to = patch_words[:, half * BANK_COLS : (half + 1) * BANK_COLS, :, :]
-                copy_from = turned_of[n][half][:].rearrange("p c u s -> p c s u")
-                bank = n * (PASS_COLS // BANK_COLS) + half
-                if bank % VECTOR_TAKES_EVERY == VECTOR_TAKES_EVERY - 1:
-                    nc.vector.tensor_copy(out=copy_to, in_=copy_from)
-                else:
-                    nc.scalar.copy(out=copy_to, in_=copy_from)
-
-        def quantise(n):
+        def quantise(group, step):
             a_codes = code_pool.tile([P, PASS_COLS * P], U32, align_bytes=64, name="a_codes")
             a_scales = code_pool.tile([P, PASS_COLS * P], U8, align_bytes=64, name="a_scales")
-            codes_of[n] = (a_codes, a_scales)
+            codes_of[(group, step)] = (a_codes, a_scales)
+            pass_patches = patches_of[group][:, step * PASS_COLS : (step + 1) * PASS_COLS, :, :]
             nc.vector.quantize_mx(
                 out=a_codes[:].bitcast(FP8X4),
                 scales=a_scales[:],
-                in_=patches_of[n][:].rearrange("p c s t -> p (c s t)"),
+                in_=pass_patches.rearrange("p c s t -> p (c s t)"),
             )
 
-        def multiply(n):
-            a_codes, a_scales = codes_of[n]
+        def multiply(group, step):
+            a_codes, a_scales = codes_of[(group, step)]
             acc = acc_psum.tile([P, PASS_COLS * P], F32, name="acc")
-            acc_of[n] = acc
+            acc_of[(group, step)] = acc
             nc.tensor.matmul_mx(
                 out=acc[:],
                 lhsT=w_codes[:].bitcast(FP8X4),
@@ -175,47 +204,86 @@ def tile_conv2d_kernel(tc, x, weights_words, weights_scales, bias, out):
                 stop=True,
             )
 
-        def finish(n):
-            sweep, pass_in_sweep = divmod(n, GROUPS * PASSES_PER_GROUP)
-            if pass_in_sweep == 0:
+        def finish(group, step):
+            sweep, group_in_sweep = divmod(group, GROUPS)
+            if group_in_sweep == 0 and step == EARLY_PASSES[0]:
                 result_of[sweep] = result_pool.tile([P, P, SEG_COLS], F32, name="result")
-            result = result_of[sweep]
-            first_col = pass_in_sweep * PASS_COLS
+            first_col = group_in_sweep * GROUP_COLS + step * PASS_COLS
             nc.scalar.activation(
-                out=result[:, :, first_col : first_col + PASS_COLS],
-                in_=acc_of[n][:].rearrange("o (c s) -> o s c", c=PASS_COLS),
+                out=result_of[sweep][:, :, first_col : first_col + PASS_COLS],
+                in_=acc_of[(group, step)][:].rearrange("o (c s) -> o s c", c=PASS_COLS),
                 func=mybir.ActivationFunctionType.Identity,
                 bias=bias_column[:, 0:1],
             )
-            if pass_in_sweep == GROUPS * PASSES_PER_GROUP - 1:
-                batch, first_image = divmod(sweep * IMAGES_PER_SWEEP, C_IN)
-                first_r = first_image * SIDE_OUT * STRIPS
-                nc.sync.dma_start(
-                    out=out[batch].rearrange("o u v -> o (u v)")[:, first_r : first_r + P * SEG_COLS],
-                    in_=result[:].rearrange("o s c -> o (s c)"),
-                )
 
-        load_image_rows(0, 0, GROUP_ROWS + TAPS - 1)
+        def store(sweep, part):
+            batch, first_image = divmod(sweep * IMAGES_PER_SWEEP, C_IN)
+            segs = P // STORE_PARTS
+            first_r = first_image * SIDE_OUT * STRIPS + part * segs * SEG_COLS
+            nc.sync.dma_start(
+                out=out[batch].rearrange("o u v -> o (u v)")[:, first_r : first_r + segs * SEG_COLS],
+                in_=result_of[sweep][:, part * segs : (part + 1) * segs, :].rearrange("o s c -> o (s c)"),
+            )
+
+        pass_order = []
+        for turn_index in range(ALL_GROUPS + 2):
+            if 0 <= turn_index - 1 < ALL_GROUPS:
+                pass_order.extend([(turn_index - 1, step) for step in EARLY_PASSES])
+            if 0 <= turn_index - 2 < ALL_GROUPS:
+                pass_order.extend([(turn_index - 2, step) for step in LATE_PASSES])
+
+        def pass_round(position):
+            if position < len(pass_order):
+                quantise(*pass_order[position])
+            if 0 <= position - 1 < len(pass_order):
+                multiply(*pass_order[position - 1])
+            if 0 <= position - 2 < len(pass_order):
+                finish(*pass_order[position - 2])
+
+        new_image(0)
+        first_rows = GROUP_ROWS + TAPS - 1
+        for row in range(first_rows):
+            for shift in range(2):
+                load_image_row(0, row, shift)
         identity = const.tile([P, P], F32)
         make_identity(nc, identity[:])
         w_codes, w_scales = load_weights(nc, const, weights_words, weights_scales)
-        load_image_rows(0, GROUP_ROWS + TAPS - 1, ROWS_LOADED)
         bias_column = bias_on_partitions(nc, const, acc_psum, identity, bias)
-        for row in range(GROUP_ROWS):
-            build_window_row(0, row)
+        for row in range(first_rows, ROWS_LOADED):
+            for shift in range(2):
+                load_image_row(0, row, shift)
+        for turned_row in range(len(TURNED_ROWS)):
+            for shift in range(2):
+                build_window(0, turned_row, shift)
 
-        for n in range(PASSES + 3):
-            group, step = divmod(n, PASSES_PER_GROUP)
-            if n < PASSES:
-                if n % (GROUPS * PASSES_PER_GROUP) == 0 and n // (GROUPS * PASSES_PER_GROUP) + 1 < SWEEPS:
-                    load_image_rows(n // (GROUPS * PASSES_PER_GROUP) + 1, 0, ROWS_LOADED)
-                turn(n)
-                copy_out(n)
-            if 0 <= n - 1 < PASSES:
-                quantise(n - 1)
-            if step < GROUP_ROWS and group + 1 < SWEEPS * GROUPS:
-                build_window_row(group + 1, step)
-            if 0 <= n - 2 < PASSES:
-                multiply(n - 2)
-            if 0 <= n - 3 < PASSES:
-                finish(n - 3)
+        position = 0
+        for group in range(ALL_GROUPS + 2):
+            sweep, group_in_sweep = divmod(group, GROUPS)
+            passes_due = len(EARLY_PASSES) * (0 <= group - 1 < ALL_GROUPS) + len(LATE_PASSES) * (0 <= group - 2 < ALL_GROUPS)
+            for bank in range(BANKS):
+                if group_in_sweep < 2 and sweep + 1 < SWEEPS:
+                    if group_in_sweep == 0 and bank == 0:
+                        new_image(sweep + 1)
+                    load_image_segments(sweep + 1, bank, group_in_sweep)
+                stored_sweep, turns_after = divmod(group - (GROUPS + 3), GROUPS)
+                if stored_sweep >= 0 and turns_after < 2 and bank % (BANKS // 2) == 0:
+                    store(stored_sweep, 2 * turns_after + bank // (BANKS // 2))
+
+                if group < ALL_GROUPS:
+                    turn(group, bank)
+                    copy_out(group, bank)
+                    cols = TURNED_COLS[bank * BANK_COLS : (bank + 1) * BANK_COLS]
+                    if COPIED_ROW * STRIPS - 1 in cols:
+                        copy_row(group, (0, 1, 2), (1, 2, 3), COPIED_ROW - 1)
+                    if (COPIED_ROW + 2) * STRIPS - 1 in cols:
+                        copy_row(group, (3,), (2,), COPIED_ROW + 1)
+                if group + 1 < ALL_GROUPS and bank < 2 * len(TURNED_ROWS):
+                    build_window(group + 1, bank // 2, bank % 2)
+                for due in range((bank + 1) * passes_due // BANKS - bank * passes_due // BANKS):
+                    pass_round(position)
+                    position += 1
+
+        pass_round(position)
+        pass_round(position + 1)
+        for part in range(STORE_PARTS):
+            store(SWEEPS - 1, part)

@@ -20,39 +20,22 @@ K = C_IN * TAPS * TAPS
 FLOPS = 2 * BATCH * SIDE_OUT * SIDE_OUT * K * C_OUT
 
 STRIPS = SIDE_OUT // C_IN
-SEG_ROWS = 20
+SEG_ROWS = 8
 SEG_COLS = SEG_ROWS * STRIPS
-SEGS_PER_IMAGE = SIDE_OUT // SEG_ROWS
-IMAGES_PER_SWEEP = P // SEGS_PER_IMAGE
-SWEEPS = BATCH * C_IN // IMAGES_PER_SWEEP
+SEGS = P // C_IN
+SWEEP_ROWS = SEGS * SEG_ROWS
+SWEEPS_PER_BATCH = SIDE_OUT // SWEEP_ROWS
+SWEEPS = BATCH * SWEEPS_PER_BATCH
 ROWS_LOADED = SEG_ROWS + TAPS - 1
 
 WORDS_USED = SIDE_OUT // 2 + 1
 WORD_PITCH = 88
 WINDOW_WORDS = WORDS_USED * 2 * TAPS
 
-GROUP_ROWS = 4
-GROUP_COLS = GROUP_ROWS * STRIPS
-GROUPS = SEG_ROWS // GROUP_ROWS
-ALL_GROUPS = SWEEPS * GROUPS
-COPIED_ROW = 1
-TURNED_ROWS = [row for row in range(GROUP_ROWS) if row != COPIED_ROW]
-TURNED_COLS = [col for col in range(GROUP_COLS) if col // STRIPS != COPIED_ROW]
-
-BANK_COLS = 2
-BANKS = (len(TURNED_COLS) + BANK_COLS - 1) // BANK_COLS
-
 PASS_COLS = 4
-PASSES_PER_GROUP = GROUP_COLS // PASS_COLS
-PASSES_PER_SWEEP = GROUPS * PASSES_PER_GROUP
-LATE_PASSES = [
-    step
-    for step in range(PASSES_PER_GROUP)
-    if step * PASS_COLS < (COPIED_ROW + 1) * STRIPS and (step + 1) * PASS_COLS > COPIED_ROW * STRIPS
-]
-EARLY_PASSES = [step for step in range(PASSES_PER_GROUP) if step not in LATE_PASSES]
-
-STORE_PARTS = 4
+PASSES_PER_SWEEP = SEG_COLS // PASS_COLS
+PASSES = SWEEPS * PASSES_PER_SWEEP
+BANK_COLS = 2
 
 VECTOR_TAKES_EVERY = 3
 
@@ -90,20 +73,20 @@ def tile_conv2d_kernel(tc, x, weights_words, weights_scales, bias, out):
     nc = tc.nc
     with ExitStack() as ctx:
         const = ctx.enter_context(tc.tile_pool(name="const", bufs=1))
-        image_pool = ctx.enter_context(tc.tile_pool(name="image", bufs=2))
-        window_pool = ctx.enter_context(tc.tile_pool(name="windows", bufs=3))
+        image_pool = ctx.enter_context(tc.tile_pool(name="image", bufs=3))
+        window_pool = ctx.enter_context(tc.tile_pool(name="windows", bufs=2))
         patch_pool = ctx.enter_context(tc.tile_pool(name="patches", bufs=3))
         code_pool = ctx.enter_context(tc.tile_pool(name="codes", bufs=3))
-        result_pool = ctx.enter_context(tc.tile_pool(name="result", bufs=2))
+        result_pool = ctx.enter_context(tc.tile_pool(name="result", bufs=3))
         turn_psum = ctx.enter_context(tc.psum_pool(name="turned", bufs=4))
         acc_psum = ctx.enter_context(tc.psum_pool(name="acc", bufs=4))
         ctx.enter_context(tc.manual_schedule())
 
         image_of = {}
-        result_of = {}
         windows_of = {}
-        patches_of = {}
+        result_of = {}
         turned_of = {}
+        patches_of = {}
         codes_of = {}
         acc_of = {}
 
@@ -111,89 +94,75 @@ def tile_conv2d_kernel(tc, x, weights_words, weights_scales, bias, out):
             image_of[sweep] = image_pool.tile([P, 2, ROWS_LOADED, 2 * WORD_PITCH], BF16, name="image")
 
         def load_image_row(sweep, row, shift):
-            batch, first_image = divmod(sweep * IMAGES_PER_SWEEP, C_IN)
+            batch, block = divmod(sweep, SWEEPS_PER_BATCH)
+            first = block * SWEEP_ROWS + row
             nc.sync.dma_start(
                 out=image_of[sweep][:, shift, row, 0 : 2 * WORDS_USED],
-                in_=x[
-                    batch,
-                    first_image : first_image + IMAGES_PER_SWEEP,
-                    row : row + (SEGS_PER_IMAGE - 1) * SEG_ROWS + 1 : SEG_ROWS,
-                    shift : shift + 2 * WORDS_USED,
-                ],
+                in_=x[batch, :, first : first + (SEGS - 1) * SEG_ROWS + 1 : SEG_ROWS, shift : shift + 2 * WORDS_USED],
             )
 
-        def load_image_segments(sweep, seg, shift):
-            batch, first_image = divmod(sweep * IMAGES_PER_SWEEP, C_IN)
+        def load_image_segment(sweep, seg, shift):
+            batch, block = divmod(sweep, SWEEPS_PER_BATCH)
+            first = block * SWEEP_ROWS + seg * SEG_ROWS
             nc.sync.dma_start(
-                out=image_of[sweep][seg:P:SEGS_PER_IMAGE, shift, :, 0 : 2 * WORDS_USED],
-                in_=x[
-                    batch,
-                    first_image : first_image + IMAGES_PER_SWEEP,
-                    seg * SEG_ROWS : seg * SEG_ROWS + ROWS_LOADED,
-                    shift : shift + 2 * WORDS_USED,
-                ],
+                out=image_of[sweep][seg:P:SEGS, shift, :, 0 : 2 * WORDS_USED],
+                in_=x[batch, :, first : first + ROWS_LOADED, shift : shift + 2 * WORDS_USED],
             )
 
-        def build_window(group, turned_row, shift):
-            sweep, group_in_sweep = divmod(group, GROUPS)
-            if turned_row == 0 and shift == 0:
-                windows_of[group] = window_pool.tile([P, len(TURNED_ROWS), WINDOW_WORDS], F32, name="windows")
-            windows_by_tap = windows_of[group][:].rearrange("p r (w e d) -> p r w e d", e=2, d=TAPS)
+        def build_windows(sweep, row, shift):
+            if row == 0 and shift == 0:
+                windows_of[sweep] = window_pool.tile([P, SEG_ROWS, WINDOW_WORDS], F32, name="windows")
+            windows_by_tap = windows_of[sweep][:].rearrange("p i (w e d) -> p i w e d", e=2, d=TAPS)
             image_words = image_of[sweep][:].bitcast(F32)
-            top = group_in_sweep * GROUP_ROWS + TURNED_ROWS[turned_row]
             nc.vector.tensor_copy(
-                out=windows_by_tap[:, turned_row, :, shift, :],
-                in_=image_words[:, shift, top : top + TAPS, 0:WORDS_USED].rearrange("p d w -> p w d"),
+                out=windows_by_tap[:, row:SEG_ROWS:TAPS, :, shift, :],
+                in_=image_words[:, shift, row : row + SEG_ROWS, 0:WORDS_USED].rearrange("p (g d) w -> p g w d", d=TAPS),
             )
 
-        def turn(group, bank):
-            turned = turn_psum.tile([P, BANK_COLS, 2, P], F32, name="turned")
-            turned_of[(group, bank)] = turned
-            for slot, col in enumerate(TURNED_COLS[bank * BANK_COLS : (bank + 1) * BANK_COLS]):
-                row, strip = divmod(col, STRIPS)
-                for pair in range(2):
-                    first_word = 2 * TAPS * (16 * strip + pair)
-                    nc.tensor.transpose(
-                        turned[:, slot, pair, :],
-                        windows_of[group][:, TURNED_ROWS.index(row), first_word : first_word + P],
-                        identity[:],
-                    )
+        def turn(n):
+            sweep, step = divmod(n, PASSES_PER_SWEEP)
+            windows = windows_of[sweep]
+            turned_of[n] = []
+            for half in range(PASS_COLS // BANK_COLS):
+                turned = turn_psum.tile([P, BANK_COLS, 2, P], F32, name="turned")
+                turned_of[n].append(turned)
+                for slot in range(BANK_COLS):
+                    row, strip = divmod(step * PASS_COLS + half * BANK_COLS + slot, STRIPS)
+                    for pair in range(2):
+                        first_word = 2 * TAPS * (16 * strip + pair)
+                        nc.tensor.transpose(
+                            turned[:, slot, pair, :],
+                            windows[:, row, first_word : first_word + P],
+                            identity[:],
+                        )
 
-        def copy_out(group, bank):
-            if bank == 0:
-                patches_of[group] = patch_pool.tile([P, GROUP_COLS, P, TAPS], BF16, align_bytes=64, name="patches")
-            patch_words = patches_of[group][:].bitcast(F32)
-            cols = TURNED_COLS[bank * BANK_COLS : (bank + 1) * BANK_COLS]
-            copy_to = patch_words[:, cols[0] : cols[-1] + 1 : max(cols[-1] - cols[0], 1), :, :]
-            copy_from = turned_of[(group, bank)][:, 0 : len(cols), :, :].rearrange("p c u s -> p c s u")
-            if (group * BANKS + bank) % VECTOR_TAKES_EVERY == VECTOR_TAKES_EVERY - 1:
-                nc.vector.tensor_copy(out=copy_to, in_=copy_from)
-            else:
-                nc.scalar.copy(out=copy_to, in_=copy_from)
+        def copy_out(n):
+            patches = patch_pool.tile([P, PASS_COLS, P, TAPS], BF16, align_bytes=64, name="patches")
+            patches_of[n] = patches
+            patch_words = patches[:].bitcast(F32)
+            for half in range(PASS_COLS // BANK_COLS):
+                copy_to = patch_words[:, half * BANK_COLS : (half + 1) * BANK_COLS, :, :]
+                copy_from = turned_of[n][half][:].rearrange("p c u s -> p c s u")
+                bank = n * (PASS_COLS // BANK_COLS) + half
+                if bank % VECTOR_TAKES_EVERY == VECTOR_TAKES_EVERY - 1:
+                    nc.vector.tensor_copy(out=copy_to, in_=copy_from)
+                else:
+                    nc.scalar.copy(out=copy_to, in_=copy_from)
 
-        def copy_row(group, taps_to, taps_from, row_from):
-            patches = patches_of[group]
-            for tap_to, tap_from in zip(taps_to, taps_from):
-                nc.sync.dma_start(
-                    out=patches[tap_to:P:TAPS, COPIED_ROW * STRIPS : (COPIED_ROW + 1) * STRIPS, :, :],
-                    in_=patches[tap_from:P:TAPS, row_from * STRIPS : (row_from + 1) * STRIPS, :, :],
-                )
-
-        def quantise(group, step):
+        def quantise(n):
             a_codes = code_pool.tile([P, PASS_COLS * P], U32, align_bytes=64, name="a_codes")
             a_scales = code_pool.tile([P, PASS_COLS * P], U8, align_bytes=64, name="a_scales")
-            codes_of[(group, step)] = (a_codes, a_scales)
-            pass_patches = patches_of[group][:, step * PASS_COLS : (step + 1) * PASS_COLS, :, :]
+            codes_of[n] = (a_codes, a_scales)
             nc.vector.quantize_mx(
                 out=a_codes[:].bitcast(FP8X4),
                 scales=a_scales[:],
-                in_=pass_patches.rearrange("p c s t -> p (c s t)"),
+                in_=patches_of[n][:].rearrange("p c s t -> p (c s t)"),
             )
 
-        def multiply(group, step):
-            a_codes, a_scales = codes_of[(group, step)]
+        def multiply(n):
+            a_codes, a_scales = codes_of[n]
             acc = acc_psum.tile([P, PASS_COLS * P], F32, name="acc")
-            acc_of[(group, step)] = acc
+            acc_of[n] = acc
             nc.tensor.matmul_mx(
                 out=acc[:],
                 lhsT=w_codes[:].bitcast(FP8X4),
@@ -204,86 +173,60 @@ def tile_conv2d_kernel(tc, x, weights_words, weights_scales, bias, out):
                 stop=True,
             )
 
-        def finish(group, step):
-            sweep, group_in_sweep = divmod(group, GROUPS)
-            if group_in_sweep == 0 and step == EARLY_PASSES[0]:
+        def finish(n):
+            sweep, step = divmod(n, PASSES_PER_SWEEP)
+            if step == 0:
                 result_of[sweep] = result_pool.tile([P, P, SEG_COLS], F32, name="result")
-            first_col = group_in_sweep * GROUP_COLS + step * PASS_COLS
+            result = result_of[sweep]
             nc.scalar.activation(
-                out=result_of[sweep][:, :, first_col : first_col + PASS_COLS],
-                in_=acc_of[(group, step)][:].rearrange("o (c s) -> o s c", c=PASS_COLS),
+                out=result[:, :, step * PASS_COLS : (step + 1) * PASS_COLS],
+                in_=acc_of[n][:].rearrange("o (c s) -> o s c", c=PASS_COLS),
                 func=mybir.ActivationFunctionType.Identity,
                 bias=bias_column[:, 0:1],
             )
-
-        def store(sweep, part):
-            batch, first_image = divmod(sweep * IMAGES_PER_SWEEP, C_IN)
-            segs = P // STORE_PARTS
-            first_r = first_image * SIDE_OUT * STRIPS + part * segs * SEG_COLS
-            nc.sync.dma_start(
-                out=out[batch].rearrange("o u v -> o (u v)")[:, first_r : first_r + segs * SEG_COLS],
-                in_=result_of[sweep][:, part * segs : (part + 1) * segs, :].rearrange("o s c -> o (s c)"),
-            )
-
-        pass_order = []
-        for turn_index in range(ALL_GROUPS + 2):
-            if 0 <= turn_index - 1 < ALL_GROUPS:
-                pass_order.extend([(turn_index - 1, step) for step in EARLY_PASSES])
-            if 0 <= turn_index - 2 < ALL_GROUPS:
-                pass_order.extend([(turn_index - 2, step) for step in LATE_PASSES])
-
-        def pass_round(position):
-            if position < len(pass_order):
-                quantise(*pass_order[position])
-            if 0 <= position - 1 < len(pass_order):
-                multiply(*pass_order[position - 1])
-            if 0 <= position - 2 < len(pass_order):
-                finish(*pass_order[position - 2])
+            if step == PASSES_PER_SWEEP - 1:
+                batch, block = divmod(sweep, SWEEPS_PER_BATCH)
+                first_r = block * SWEEP_ROWS * STRIPS
+                nc.sync.dma_start(
+                    out=out[batch].rearrange("o u v -> o (u v)").rearrange("o (c r) -> o c r", c=C_IN)[
+                        :, :, first_r : first_r + SEGS * SEG_COLS
+                    ],
+                    in_=result[:].rearrange("o (c g) k -> o c (g k)", g=SEGS),
+                )
 
         new_image(0)
-        first_rows = GROUP_ROWS + TAPS - 1
-        for row in range(first_rows):
+        for row in range(SEG_ROWS):
             for shift in range(2):
                 load_image_row(0, row, shift)
         identity = const.tile([P, P], F32)
         make_identity(nc, identity[:])
         w_codes, w_scales = load_weights(nc, const, weights_words, weights_scales)
         bias_column = bias_on_partitions(nc, const, acc_psum, identity, bias)
-        for row in range(first_rows, ROWS_LOADED):
+        for row in range(SEG_ROWS, ROWS_LOADED):
             for shift in range(2):
                 load_image_row(0, row, shift)
-        for turned_row in range(len(TURNED_ROWS)):
+        new_image(1)
+        for seg in range(SEGS):
             for shift in range(2):
-                build_window(0, turned_row, shift)
+                load_image_segment(1, seg, shift)
+        for row in range(TAPS):
+            for shift in range(2):
+                build_windows(0, row, shift)
 
-        position = 0
-        for group in range(ALL_GROUPS + 2):
-            sweep, group_in_sweep = divmod(group, GROUPS)
-            passes_due = len(EARLY_PASSES) * (0 <= group - 1 < ALL_GROUPS) + len(LATE_PASSES) * (0 <= group - 2 < ALL_GROUPS)
-            for bank in range(BANKS):
-                if group_in_sweep < 2 and sweep + 1 < SWEEPS:
-                    if group_in_sweep == 0 and bank == 0:
-                        new_image(sweep + 1)
-                    load_image_segments(sweep + 1, bank, group_in_sweep)
-                stored_sweep, turns_after = divmod(group - (GROUPS + 3), GROUPS)
-                if stored_sweep >= 0 and turns_after < 2 and bank % (BANKS // 2) == 0:
-                    store(stored_sweep, 2 * turns_after + bank // (BANKS // 2))
-
-                if group < ALL_GROUPS:
-                    turn(group, bank)
-                    copy_out(group, bank)
-                    cols = TURNED_COLS[bank * BANK_COLS : (bank + 1) * BANK_COLS]
-                    if COPIED_ROW * STRIPS - 1 in cols:
-                        copy_row(group, (0, 1, 2), (1, 2, 3), COPIED_ROW - 1)
-                    if (COPIED_ROW + 2) * STRIPS - 1 in cols:
-                        copy_row(group, (3,), (2,), COPIED_ROW + 1)
-                if group + 1 < ALL_GROUPS and bank < 2 * len(TURNED_ROWS):
-                    build_window(group + 1, bank // 2, bank % 2)
-                for due in range((bank + 1) * passes_due // BANKS - bank * passes_due // BANKS):
-                    pass_round(position)
-                    position += 1
-
-        pass_round(position)
-        pass_round(position + 1)
-        for part in range(STORE_PARTS):
-            store(SWEEPS - 1, part)
+        for n in range(PASSES + 3):
+            sweep, step = divmod(n, PASSES_PER_SWEEP)
+            if step < 2 * SEGS and sweep + 2 < SWEEPS:
+                if step == 0:
+                    new_image(sweep + 2)
+                load_image_segment(sweep + 2, step // 2, step % 2)
+            if n < PASSES:
+                turn(n)
+                copy_out(n)
+            if 0 <= n - 1 < PASSES:
+                quantise(n - 1)
+            if step < 2 * TAPS and sweep + 1 < SWEEPS:
+                build_windows(sweep + 1, step // 2, step % 2)
+            if 0 <= n - 2 < PASSES:
+                multiply(n - 2)
+            if 0 <= n - 3 < PASSES:
+                finish(n - 3)

@@ -33,9 +33,15 @@ WORD_PITCH = 88
 WINDOW_WORDS = WORDS_USED * 2 * TAPS
 
 PASS_COLS = 4
-PASSES_PER_SWEEP = SEG_COLS // PASS_COLS
-PASSES = SWEEPS * PASSES_PER_SWEEP
+STEP_PASSES = 2
+STEP_COLS = STEP_PASSES * PASS_COLS
+STEPS_PER_SWEEP = SEG_COLS // STEP_COLS
+STEPS = SWEEPS * STEPS_PER_SWEEP
 BANK_COLS = 2
+STEP_BANKS = STEP_COLS // BANK_COLS
+
+TURNED_BANKS = 6
+ACC_BANKS = 2
 
 VECTOR_TAKES_EVERY = 3
 
@@ -78,8 +84,8 @@ def tile_conv2d_kernel(tc, x, weights_words, weights_scales, bias, out):
         patch_pool = ctx.enter_context(tc.tile_pool(name="patches", bufs=3))
         code_pool = ctx.enter_context(tc.tile_pool(name="codes", bufs=3))
         result_pool = ctx.enter_context(tc.tile_pool(name="result", bufs=3))
-        turn_psum = ctx.enter_context(tc.psum_pool(name="turned", bufs=4))
-        acc_psum = ctx.enter_context(tc.psum_pool(name="acc", bufs=4))
+        turn_psum = ctx.enter_context(tc.psum_pool(name="turned", bufs=TURNED_BANKS))
+        acc_psum = ctx.enter_context(tc.psum_pool(name="acc", bufs=ACC_BANKS))
         ctx.enter_context(tc.manual_schedule())
 
         image_of = {}
@@ -92,14 +98,6 @@ def tile_conv2d_kernel(tc, x, weights_words, weights_scales, bias, out):
 
         def new_image(sweep):
             image_of[sweep] = image_pool.tile([P, 2, ROWS_LOADED, 2 * WORD_PITCH], BF16, name="image")
-
-        def load_image_row(sweep, row, shift):
-            batch, block = divmod(sweep, SWEEPS_PER_BATCH)
-            first = block * SWEEP_ROWS + row
-            nc.sync.dma_start(
-                out=image_of[sweep][:, shift, row, 0 : 2 * WORDS_USED],
-                in_=x[batch, :, first : first + (SEGS - 1) * SEG_ROWS + 1 : SEG_ROWS, shift : shift + 2 * WORDS_USED],
-            )
 
         def load_image_segment(sweep, seg, shift):
             batch, block = divmod(sweep, SWEEPS_PER_BATCH)
@@ -120,14 +118,14 @@ def tile_conv2d_kernel(tc, x, weights_words, weights_scales, bias, out):
             )
 
         def turn(n):
-            sweep, step = divmod(n, PASSES_PER_SWEEP)
+            sweep, step = divmod(n, STEPS_PER_SWEEP)
             windows = windows_of[sweep]
             turned_of[n] = []
-            for half in range(PASS_COLS // BANK_COLS):
+            for bank in range(STEP_BANKS):
                 turned = turn_psum.tile([P, BANK_COLS, 2, P], F32, name="turned")
                 turned_of[n].append(turned)
                 for slot in range(BANK_COLS):
-                    row, strip = divmod(step * PASS_COLS + half * BANK_COLS + slot, STRIPS)
+                    row, strip = divmod(step * STEP_COLS + bank * BANK_COLS + slot, STRIPS)
                     for pair in range(2):
                         first_word = 2 * TAPS * (16 * strip + pair)
                         nc.tensor.transpose(
@@ -137,21 +135,20 @@ def tile_conv2d_kernel(tc, x, weights_words, weights_scales, bias, out):
                         )
 
         def copy_out(n):
-            patches = patch_pool.tile([P, PASS_COLS, P, TAPS], BF16, align_bytes=64, name="patches")
+            patches = patch_pool.tile([P, STEP_COLS, P, TAPS], BF16, align_bytes=64, name="patches")
             patches_of[n] = patches
             patch_words = patches[:].bitcast(F32)
-            for half in range(PASS_COLS // BANK_COLS):
-                copy_to = patch_words[:, half * BANK_COLS : (half + 1) * BANK_COLS, :, :]
-                copy_from = turned_of[n][half][:].rearrange("p c u s -> p c s u")
-                bank = n * (PASS_COLS // BANK_COLS) + half
-                if bank % VECTOR_TAKES_EVERY == VECTOR_TAKES_EVERY - 1:
+            for bank in range(STEP_BANKS):
+                copy_to = patch_words[:, bank * BANK_COLS : (bank + 1) * BANK_COLS, :, :]
+                copy_from = turned_of[n][bank][:].rearrange("p c u s -> p c s u")
+                if (n * STEP_BANKS + bank) % VECTOR_TAKES_EVERY == VECTOR_TAKES_EVERY - 1:
                     nc.vector.tensor_copy(out=copy_to, in_=copy_from)
                 else:
                     nc.scalar.copy(out=copy_to, in_=copy_from)
 
         def quantise(n):
-            a_codes = code_pool.tile([P, PASS_COLS * P], U32, align_bytes=64, name="a_codes")
-            a_scales = code_pool.tile([P, PASS_COLS * P], U8, align_bytes=64, name="a_scales")
+            a_codes = code_pool.tile([P, STEP_COLS * P], U32, align_bytes=64, name="a_codes")
+            a_scales = code_pool.tile([P, STEP_COLS * P], U8, align_bytes=64, name="a_scales")
             codes_of[n] = (a_codes, a_scales)
             nc.vector.quantize_mx(
                 out=a_codes[:].bitcast(FP8X4),
@@ -161,30 +158,35 @@ def tile_conv2d_kernel(tc, x, weights_words, weights_scales, bias, out):
 
         def multiply(n):
             a_codes, a_scales = codes_of[n]
-            acc = acc_psum.tile([P, PASS_COLS * P], F32, name="acc")
-            acc_of[n] = acc
-            nc.tensor.matmul_mx(
-                out=acc[:],
-                lhsT=w_codes[:].bitcast(FP8X4),
-                lhsT_scale=w_scales[:],
-                rhs=a_codes[:].bitcast(FP8X4),
-                rhs_scale=a_scales[:],
-                start=True,
-                stop=True,
-            )
+            acc_of[n] = []
+            for half in range(STEP_PASSES):
+                acc = acc_psum.tile([P, PASS_COLS * P], F32, name="acc")
+                acc_of[n].append(acc)
+                moving = slice(half * PASS_COLS * P, (half + 1) * PASS_COLS * P)
+                nc.tensor.matmul_mx(
+                    out=acc[:],
+                    lhsT=w_codes[:].bitcast(FP8X4),
+                    lhsT_scale=w_scales[:],
+                    rhs=a_codes[:, moving].bitcast(FP8X4),
+                    rhs_scale=a_scales[:, moving],
+                    start=True,
+                    stop=True,
+                )
 
         def finish(n):
-            sweep, step = divmod(n, PASSES_PER_SWEEP)
+            sweep, step = divmod(n, STEPS_PER_SWEEP)
             if step == 0:
                 result_of[sweep] = result_pool.tile([P, P, SEG_COLS], F32, name="result")
             result = result_of[sweep]
-            nc.scalar.activation(
-                out=result[:, :, step * PASS_COLS : (step + 1) * PASS_COLS],
-                in_=acc_of[n][:].rearrange("o (c s) -> o s c", c=PASS_COLS),
-                func=mybir.ActivationFunctionType.Identity,
-                bias=bias_column[:, 0:1],
-            )
-            if step == PASSES_PER_SWEEP - 1:
+            for half in range(STEP_PASSES):
+                first_col = step * STEP_COLS + half * PASS_COLS
+                nc.scalar.activation(
+                    out=result[:, :, first_col : first_col + PASS_COLS],
+                    in_=acc_of[n][half][:].rearrange("o (c s) -> o s c", c=PASS_COLS),
+                    func=mybir.ActivationFunctionType.Identity,
+                    bias=bias_column[:, 0:1],
+                )
+            if step == STEPS_PER_SWEEP - 1:
                 batch, block = divmod(sweep, SWEEPS_PER_BATCH)
                 first_r = block * SWEEP_ROWS * STRIPS
                 nc.sync.dma_start(
@@ -194,39 +196,36 @@ def tile_conv2d_kernel(tc, x, weights_words, weights_scales, bias, out):
                     in_=result[:].rearrange("o (c g) k -> o c (g k)", g=SEGS),
                 )
 
-        new_image(0)
-        for row in range(SEG_ROWS):
-            for shift in range(2):
-                load_image_row(0, row, shift)
         identity = const.tile([P, P], F32)
         make_identity(nc, identity[:])
-        w_codes, w_scales = load_weights(nc, const, weights_words, weights_scales)
         bias_column = bias_on_partitions(nc, const, acc_psum, identity, bias)
-        for row in range(SEG_ROWS, ROWS_LOADED):
-            for shift in range(2):
-                load_image_row(0, row, shift)
-        new_image(1)
-        for seg in range(SEGS):
-            for shift in range(2):
-                load_image_segment(1, seg, shift)
+        for sweep in range(2):
+            new_image(sweep)
+            for seg in range(SEGS):
+                for shift in range(2):
+                    load_image_segment(sweep, seg, shift)
+            if sweep == 0:
+                w_codes, w_scales = load_weights(nc, const, weights_words, weights_scales)
         for row in range(TAPS):
             for shift in range(2):
                 build_windows(0, row, shift)
 
-        for n in range(PASSES + 3):
-            sweep, step = divmod(n, PASSES_PER_SWEEP)
-            if step < 2 * SEGS and sweep + 2 < SWEEPS:
+        for n in range(STEPS + 3):
+            sweep, step = divmod(n, STEPS_PER_SWEEP)
+            if 0 <= n - 3 < STEPS:
+                finish(n - 3)
+            if step < SEGS and sweep + 2 < SWEEPS:
                 if step == 0:
                     new_image(sweep + 2)
-                load_image_segment(sweep + 2, step // 2, step % 2)
-            if n < PASSES:
+                for shift in range(2):
+                    load_image_segment(sweep + 2, step, shift)
+            if n < STEPS:
                 turn(n)
                 copy_out(n)
-            if 0 <= n - 1 < PASSES:
+            if 0 <= n - 1 < STEPS:
                 quantise(n - 1)
-            if step < 2 * TAPS and sweep + 1 < SWEEPS:
-                build_windows(sweep + 1, step // 2, step % 2)
-            if 0 <= n - 2 < PASSES:
+            if step < TAPS and sweep + 1 < SWEEPS:
+                for shift in range(2):
+                    build_windows(sweep + 1, step, shift)
+            if 0 <= n - 2 < STEPS:
                 multiply(n - 2)
-            if 0 <= n - 3 < PASSES:
-                finish(n - 3)

@@ -43,7 +43,7 @@ STEP_BANKS = STEP_COLS // BANK_COLS
 TURNED_BANKS = 6
 ACC_BANKS = 2
 
-VECTOR_TAKES_EVERY = 3
+VECTOR_TAKES_EVERY = 4
 
 
 def load_weights(nc, const, weights_words, weights_scales):

@@ -15,217 +15,223 @@ BATCH = 2
 C_IN = 32
 SIDE_OUT = 160
 TAPS = 4
+SIDE_IN = SIDE_OUT + TAPS - 1
 C_OUT = 128
 K = C_IN * TAPS * TAPS
 FLOPS = 2 * BATCH * SIDE_OUT * SIDE_OUT * K * C_OUT
 
 STRIPS = SIDE_OUT // C_IN
-SEG_ROWS = 8
-SEG_COLS = SEG_ROWS * STRIPS
-SEGS = P // C_IN
-SWEEP_ROWS = SEGS * SEG_ROWS
-SWEEPS_PER_BATCH = SIDE_OUT // SWEEP_ROWS
-SWEEPS = BATCH * SWEEPS_PER_BATCH
-ROWS_LOADED = SEG_ROWS + TAPS - 1
+ALL_ROWS = BATCH * C_IN * SIDE_IN
+CHUNKS = 4
+GROUP_ROWS = CHUNKS * P
+WORDS = GROUP_ROWS // TAPS
+VERSIONS = TAPS
+VERSION_LEN = STRIPS * GROUP_ROWS
+PAIR_LEN = 2 * VERSION_LEN
+UNITS = VERSIONS * STRIPS
+PASS_UNITS = 4
+PASSES = UNITS // PASS_UNITS
+STORE_ROWS = 8
 
-WORDS_USED = SIDE_OUT // 2 + 1
-WORD_PITCH = 88
-WINDOW_WORDS = WORDS_USED * 2 * TAPS
-
-PASS_COLS = 4
-STEP_PASSES = 2
-STEP_COLS = STEP_PASSES * PASS_COLS
-STEPS_PER_SWEEP = SEG_COLS // STEP_COLS
-STEPS = SWEEPS * STEPS_PER_SWEEP
-BANK_COLS = 2
-STEP_BANKS = STEP_COLS // BANK_COLS
-
-TURNED_BANKS = 6
-ACC_BANKS = 2
-
-VECTOR_TAKES_EVERY = 4
+BANK_STRIPS = 2
+TURNED_BANKS = 3
+ACC_BANKS = PASSES
+TAIL = 32
 
 
-def load_weights(nc, const, weights_words, weights_scales):
+def plan_groups():
+    groups = []
+    end = ALL_ROWS - (TAPS - 1)
+    start = 0
+    while start < end:
+        stop = min(start + GROUP_ROWS - (TAPS - 1), end)
+        if stop < end:
+            row = stop % SIDE_IN
+            stop -= row % STORE_ROWS if row <= SIDE_OUT else row - SIDE_OUT
+        groups.append((min(start, ALL_ROWS - GROUP_ROWS), start, stop))
+        start = stop + (TAPS - 1 if stop % SIDE_IN == SIDE_OUT else 0)
+    return groups
+
+
+def load_weight_codes(nc, const, weights_words):
     w_codes = const.tile([P, 4 * C_OUT], U8, align_bytes=64)
     nc.sync.dma_start(
         out=w_codes[:].bitcast(I32),
         in_=weights_words[0].rearrange("p n t -> p (n t)").bitcast(I32),
     )
-    w_scales = const.tile([P, C_OUT], U8, align_bytes=64)
-    nc.vector.memset(w_scales[:].bitcast(I32), 0)
+    return w_codes
+
+
+def load_weight_scales(nc, w_scales, weights_scales):
     for quadrant in range(4):
         nc.sync.dma_start(
             out=w_scales[32 * quadrant : 32 * quadrant + 4, :].bitcast(I32),
             in_=weights_scales[0, 4 * quadrant : 4 * quadrant + 4, :].bitcast(I32),
         )
-    return w_codes, w_scales
 
 
-def bias_on_partitions(nc, const, acc_psum, identity, bias):
-    bias_row = const.tile([1, C_OUT], BF16)
-    nc.scalar.dma_start(out=bias_row[:], in_=bias.unsqueeze(0))
-    bias_square = const.tile([P, C_OUT], F32)
+def bias_on_partitions(nc, const, turn_psum, identity, bias):
+    bias_square = const.tile([P, C_OUT], BF16)
     nc.vector.memset(bias_square[:], 0.0)
-    nc.vector.tensor_copy(out=bias_square[0:1, :], in_=bias_row[:])
-    bias_turned = acc_psum.tile([P, PASS_COLS * P], F32, tag="acc")
-    nc.tensor.transpose(bias_turned[:, 0:P], bias_square[:], identity[:])
+    nc.scalar.dma_start(out=bias_square[0:1, :], in_=bias.unsqueeze(0))
+    bias_turned = turn_psum.tile([P, BANK_STRIPS, CHUNKS, P], BF16, name="turned")
+    nc.tensor.transpose(bias_turned[:, 0, 0, :], bias_square[:], identity[:])
     bias_column = const.tile([P, 1], F32)
-    nc.vector.tensor_copy(out=bias_column[:], in_=bias_turned[:, 0:1])
+    nc.vector.tensor_copy(out=bias_column[:], in_=bias_turned[:, 0, 0, 0:1])
     return bias_column
 
 
 def tile_conv2d_kernel(tc, x, weights_words, weights_scales, bias, out):
     nc = tc.nc
+    groups = plan_groups()
+    n_groups = len(groups)
+    x_rows = x.rearrange("b c h w -> (b c h) w")
     with ExitStack() as ctx:
         const = ctx.enter_context(tc.tile_pool(name="const", bufs=1))
-        image_pool = ctx.enter_context(tc.tile_pool(name="image", bufs=3))
+        rows_pool = ctx.enter_context(tc.tile_pool(name="rows", bufs=4))
         window_pool = ctx.enter_context(tc.tile_pool(name="windows", bufs=2))
-        patch_pool = ctx.enter_context(tc.tile_pool(name="patches", bufs=3))
+        version_pool = ctx.enter_context(tc.tile_pool(name="versions", bufs=3))
         code_pool = ctx.enter_context(tc.tile_pool(name="codes", bufs=3))
         result_pool = ctx.enter_context(tc.tile_pool(name="result", bufs=3))
         turn_psum = ctx.enter_context(tc.psum_pool(name="turned", bufs=TURNED_BANKS))
         acc_psum = ctx.enter_context(tc.psum_pool(name="acc", bufs=ACC_BANKS))
         ctx.enter_context(tc.manual_schedule())
 
-        image_of = {}
+        rows_of = {}
         windows_of = {}
-        result_of = {}
-        turned_of = {}
-        patches_of = {}
+        versions_of = {}
         codes_of = {}
-        acc_of = {}
 
-        def new_image(sweep):
-            image_of[sweep] = image_pool.tile([P, 2, ROWS_LOADED, 2 * WORD_PITCH], BF16, name="image")
+        def load_rows(n):
+            base = groups[n][0]
+            rows = rows_pool.tile([P, TAPS, CHUNKS, SIDE_OUT], BF16, name="rows")
+            rows_of[n] = rows
+            for e in range(2):
+                for pair in range(2):
+                    first = 2 * pair + e
+                    nc.sync.dma_start(
+                        out=rows[:, 2 * e + pair, :, :],
+                        in_=x_rows[base : base + GROUP_ROWS, first : first + SIDE_OUT].rearrange("(k p) w -> p k w", p=P),
+                    )
 
-        def load_image_segment(sweep, seg, shift):
-            batch, block = divmod(sweep, SWEEPS_PER_BATCH)
-            first = block * SWEEP_ROWS + seg * SEG_ROWS
-            nc.sync.dma_start(
-                out=image_of[sweep][seg:P:SEGS, shift, :, 0 : 2 * WORDS_USED],
-                in_=x[batch, :, first : first + ROWS_LOADED, shift : shift + 2 * WORDS_USED],
-            )
-
-        def build_windows(sweep, row, shift):
-            if row == 0 and shift == 0:
-                windows_of[sweep] = window_pool.tile([P, SEG_ROWS, WINDOW_WORDS], F32, name="windows")
-            windows_by_tap = windows_of[sweep][:].rearrange("p i (w e d) -> p i w e d", e=2, d=TAPS)
-            image_words = image_of[sweep][:].bitcast(F32)
+        def build_windows(n):
+            windows = window_pool.tile([P, CHUNKS, STRIPS * P], BF16, name="windows")
+            windows_of[n] = windows
             nc.vector.tensor_copy(
-                out=windows_by_tap[:, row:SEG_ROWS:TAPS, :, shift, :],
-                in_=image_words[:, shift, row : row + SEG_ROWS, 0:WORDS_USED].rearrange("p (g d) w -> p g w d", d=TAPS),
+                out=windows[:].bitcast(F32).rearrange("p k (w f) -> p k w f", f=TAPS),
+                in_=rows_of[n][:].bitcast(F32).rearrange("p f k w -> p k w f"),
             )
 
-        def turn(n):
-            sweep, step = divmod(n, STEPS_PER_SWEEP)
-            windows = windows_of[sweep]
-            turned_of[n] = []
-            for bank in range(STEP_BANKS):
-                turned = turn_psum.tile([P, BANK_COLS, 2, P], F32, name="turned")
-                turned_of[n].append(turned)
-                for slot in range(BANK_COLS):
-                    row, strip = divmod(step * STEP_COLS + bank * BANK_COLS + slot, STRIPS)
-                    for pair in range(2):
-                        first_word = 2 * TAPS * (16 * strip + pair)
+        def turn_and_seed(n):
+            low = version_pool.tile([P, PAIR_LEN], BF16, align_bytes=64, name="low")
+            high = version_pool.tile([P, PAIR_LEN], BF16, align_bytes=64, name="high")
+            versions_of[n] = (low, high)
+            nc.gpsimd.memset(low[:, PAIR_LEN - TAIL : PAIR_LEN], 0.0)
+            nc.gpsimd.memset(high[:].rearrange("p (r g) -> p r g", g=GROUP_ROWS)[:, :, GROUP_ROWS - TAIL : GROUP_ROWS], 0.0)
+            windows = windows_of[n]
+            for bank in range(TURNED_BANKS):
+                strips = range(bank * BANK_STRIPS, min((bank + 1) * BANK_STRIPS, STRIPS))
+                turned = turn_psum.tile([P, BANK_STRIPS, CHUNKS, P], BF16, name="turned")
+                for strip in strips:
+                    for chunk in range(CHUNKS):
                         nc.tensor.transpose(
-                            turned[:, slot, pair, :],
-                            windows[:, row, first_word : first_word + P],
+                            turned[:, strip % BANK_STRIPS, chunk, :],
+                            windows[:, chunk, strip * P : (strip + 1) * P],
                             identity[:],
                         )
+                flat = turned[:].rearrange("p s k g -> p (s k g)")
+                first = bank * BANK_STRIPS * GROUP_ROWS
+                length = len(strips) * GROUP_ROWS
+                nc.scalar.copy(out=low[:, first : first + length], in_=flat[:, 0:length])
+                nc.scalar.copy(out=high[:, first : first + length - 2], in_=flat[:, 2:length])
 
-        def copy_out(n):
-            patches = patch_pool.tile([P, STEP_COLS, P, TAPS], BF16, align_bytes=64, name="patches")
-            patches_of[n] = patches
-            patch_words = patches[:].bitcast(F32)
-            for bank in range(STEP_BANKS):
-                copy_to = patch_words[:, bank * BANK_COLS : (bank + 1) * BANK_COLS, :, :]
-                copy_from = turned_of[n][bank][:].rearrange("p c u s -> p c s u")
-                if (n * STEP_BANKS + bank) % VECTOR_TAKES_EVERY == VECTOR_TAKES_EVERY - 1:
-                    nc.vector.tensor_copy(out=copy_to, in_=copy_from)
-                else:
-                    nc.scalar.copy(out=copy_to, in_=copy_from)
+        def odd_versions(n):
+            low, high = versions_of[n]
+            nc.vector.tensor_copy(out=low[:, VERSION_LEN : PAIR_LEN - 1], in_=low[:, 1:VERSION_LEN])
+            nc.vector.tensor_copy(out=high[:, VERSION_LEN : PAIR_LEN - 2], in_=low[:, VERSION_LEN + 2 : PAIR_LEN])
 
         def quantise(n):
-            a_codes = code_pool.tile([P, STEP_COLS * P], U32, align_bytes=64, name="a_codes")
-            a_scales = code_pool.tile([P, STEP_COLS * P], U8, align_bytes=64, name="a_scales")
+            a_codes = code_pool.tile([P, UNITS * WORDS], U32, align_bytes=64, name="a_codes")
+            a_scales = code_pool.tile([P, UNITS * WORDS], U8, align_bytes=64, name="a_scales")
             codes_of[n] = (a_codes, a_scales)
-            nc.vector.quantize_mx(
-                out=a_codes[:].bitcast(FP8X4),
-                scales=a_scales[:],
-                in_=patches_of[n][:].rearrange("p c s t -> p (c s t)"),
-            )
+            for half, values in enumerate(versions_of[n]):
+                for first, last in ((0, 4096), (4096, PAIR_LEN)):
+                    words = slice((half * PAIR_LEN + first) // TAPS, (half * PAIR_LEN + last) // TAPS)
+                    nc.vector.quantize_mx(
+                        out=a_codes[:, words].bitcast(FP8X4),
+                        scales=a_scales[:, words],
+                        in_=values[:, first:last],
+                    )
 
-        def multiply(n):
+        def multiply_and_store(n):
             a_codes, a_scales = codes_of[n]
-            acc_of[n] = []
-            for half in range(STEP_PASSES):
-                acc = acc_psum.tile([P, PASS_COLS * P], F32, name="acc")
-                acc_of[n].append(acc)
-                moving = slice(half * PASS_COLS * P, (half + 1) * PASS_COLS * P)
+            result = result_pool.tile([P, WORDS * UNITS], F32, name="result")
+            result_by_unit = result[:].rearrange("o (j u) -> o j u", u=UNITS)
+            accs = []
+            for z in range(PASSES):
+                acc = acc_psum.tile([P, PASS_UNITS * WORDS], F32, name="acc")
+                accs.append(acc)
+                moving = slice(z * PASS_UNITS * WORDS, (z + 1) * PASS_UNITS * WORDS)
                 nc.tensor.matmul_mx(
                     out=acc[:],
-                    lhsT=w_codes[:].bitcast(FP8X4),
+                    lhsT=w_swapped[:].bitcast(FP8X4),
                     lhsT_scale=w_scales[:],
                     rhs=a_codes[:, moving].bitcast(FP8X4),
                     rhs_scale=a_scales[:, moving],
                     start=True,
                     stop=True,
                 )
-
-        def finish(n):
-            sweep, step = divmod(n, STEPS_PER_SWEEP)
-            if step == 0:
-                result_of[sweep] = result_pool.tile([P, P, SEG_COLS], F32, name="result")
-            result = result_of[sweep]
-            for half in range(STEP_PASSES):
-                first_col = step * STEP_COLS + half * PASS_COLS
+            for z in range(PASSES):
                 nc.scalar.activation(
-                    out=result[:, :, first_col : first_col + PASS_COLS],
-                    in_=acc_of[n][half][:].rearrange("o (c s) -> o s c", c=PASS_COLS),
+                    out=result_by_unit[:, :, z * PASS_UNITS : (z + 1) * PASS_UNITS],
+                    in_=accs[z][:].rearrange("o (u j) -> o j u", u=PASS_UNITS),
                     func=mybir.ActivationFunctionType.Identity,
                     bias=bias_column[:, 0:1],
                 )
-            if step == STEPS_PER_SWEEP - 1:
-                batch, block = divmod(sweep, SWEEPS_PER_BATCH)
-                first_r = block * SWEEP_ROWS * STRIPS
+            base, g, stop = groups[n]
+            while g < stop:
+                image, row = divmod(g, SIDE_IN)
+                g_end = min(stop, image * SIDE_IN + SIDE_OUT)
+                batch, channel = divmod(image, C_IN)
+                first_r = (channel * SIDE_OUT + row) * STRIPS
+                count = (g_end - g) * STRIPS
                 nc.sync.dma_start(
-                    out=out[batch].rearrange("o u v -> o (u v)").rearrange("o (c r) -> o c r", c=C_IN)[
-                        :, :, first_r : first_r + SEGS * SEG_COLS
-                    ],
-                    in_=result[:].rearrange("o (c g) k -> o c (g k)", g=SEGS),
+                    out=out[batch].rearrange("o u v -> o (u v)")[:, first_r : first_r + count],
+                    in_=result[:, (g - base) * STRIPS : (g - base) * STRIPS + count],
                 )
+                g = g_end + TAPS - 1
 
-        identity = const.tile([P, P], F32)
+        identity = const.tile([P, P], BF16)
         make_identity(nc, identity[:])
-        bias_column = bias_on_partitions(nc, const, acc_psum, identity, bias)
-        for sweep in range(2):
-            new_image(sweep)
-            for seg in range(SEGS):
-                for shift in range(2):
-                    load_image_segment(sweep, seg, shift)
-            if sweep == 0:
-                w_codes, w_scales = load_weights(nc, const, weights_words, weights_scales)
-        for row in range(TAPS):
-            for shift in range(2):
-                build_windows(0, row, shift)
+        w_scales = const.tile([P, C_OUT], U8, align_bytes=64)
+        nc.vector.memset(w_scales[:].bitcast(I32), 0)
+        w_codes = load_weight_codes(nc, const, weights_words)
+        load_rows(0)
+        load_weight_scales(nc, w_scales, weights_scales)
+        bias_column = bias_on_partitions(nc, const, turn_psum, identity, bias)
+        w_planes = const.tile([P, TAPS, C_OUT], U8, align_bytes=64)
+        nc.vector.tensor_copy(out=w_planes[:], in_=w_codes[:].rearrange("p (n t) -> p t n", t=TAPS))
+        w_moved = const.tile([P, TAPS, C_OUT], U8, align_bytes=64)
+        for di in range(TAPS):
+            for dj in range(TAPS):
+                nc.sync.dma_start(out=w_moved[dj:P:TAPS, di, :].bitcast(I32), in_=w_planes[di:P:TAPS, dj, :].bitcast(I32))
+        load_rows(1)
+        load_rows(2)
+        build_windows(0)
+        w_swapped = const.tile([P, TAPS * C_OUT], U8, align_bytes=64)
+        nc.vector.tensor_copy(
+            out=w_swapped[:].rearrange("p (n t) -> p n t", t=TAPS), in_=w_moved[:].rearrange("p t n -> p n t")
+        )
 
-        for n in range(STEPS + 3):
-            sweep, step = divmod(n, STEPS_PER_SWEEP)
-            if 0 <= n - 3 < STEPS:
-                finish(n - 3)
-            if step < SEGS and sweep + 2 < SWEEPS:
-                if step == 0:
-                    new_image(sweep + 2)
-                for shift in range(2):
-                    load_image_segment(sweep + 2, step, shift)
-            if n < STEPS:
-                turn(n)
-                copy_out(n)
-            if 0 <= n - 1 < STEPS:
+        for n in range(n_groups + 2):
+            if n + 3 < n_groups:
+                load_rows(n + 3)
+            if n + 1 < n_groups:
+                build_windows(n + 1)
+            if n < n_groups:
+                turn_and_seed(n)
+            if 0 <= n - 1 < n_groups:
+                odd_versions(n - 1)
                 quantise(n - 1)
-            if step < TAPS and sweep + 1 < SWEEPS:
-                for shift in range(2):
-                    build_windows(sweep + 1, step, shift)
-            if 0 <= n - 2 < STEPS:
-                multiply(n - 2)
+            if 0 <= n - 2 < n_groups:
+                multiply_and_store(n - 2)

@@ -36,6 +36,7 @@ STORE_ROWS = 8
 BANK_STRIPS = 2
 TURNED_BANKS = 3
 ACC_BANKS = PASSES
+VERSION_TILES = 3
 TAIL = 32
 
 
@@ -90,7 +91,6 @@ def tile_conv2d_kernel(tc, x, weights_words, weights_scales, bias, out):
         const = ctx.enter_context(tc.tile_pool(name="const", bufs=1))
         rows_pool = ctx.enter_context(tc.tile_pool(name="rows", bufs=4))
         window_pool = ctx.enter_context(tc.tile_pool(name="windows", bufs=2))
-        version_pool = ctx.enter_context(tc.tile_pool(name="versions", bufs=3))
         code_pool = ctx.enter_context(tc.tile_pool(name="codes", bufs=3))
         result_pool = ctx.enter_context(tc.tile_pool(name="result", bufs=3))
         turn_psum = ctx.enter_context(tc.psum_pool(name="turned", bufs=TURNED_BANKS))
@@ -123,11 +123,8 @@ def tile_conv2d_kernel(tc, x, weights_words, weights_scales, bias, out):
             )
 
         def turn_and_seed(n):
-            low = version_pool.tile([P, PAIR_LEN], BF16, align_bytes=64, name="low")
-            high = version_pool.tile([P, PAIR_LEN], BF16, align_bytes=64, name="high")
+            low, high = version_tiles[n % VERSION_TILES]
             versions_of[n] = (low, high)
-            nc.gpsimd.memset(low[:, PAIR_LEN - TAIL : PAIR_LEN], 0.0)
-            nc.gpsimd.memset(high[:].rearrange("p (r g) -> p r g", g=GROUP_ROWS)[:, :, GROUP_ROWS - TAIL : GROUP_ROWS], 0.0)
             windows = windows_of[n]
             for bank in range(TURNED_BANKS):
                 strips = range(bank * BANK_STRIPS, min((bank + 1) * BANK_STRIPS, STRIPS))
@@ -222,6 +219,14 @@ def tile_conv2d_kernel(tc, x, weights_words, weights_scales, bias, out):
         nc.vector.tensor_copy(
             out=w_swapped[:].rearrange("p (n t) -> p n t", t=TAPS), in_=w_moved[:].rearrange("p t n -> p n t")
         )
+
+        version_tiles = []
+        for turn in range(VERSION_TILES):
+            low = const.tile([P, PAIR_LEN], BF16, align_bytes=64, name="low%d" % turn)
+            high = const.tile([P, PAIR_LEN], BF16, align_bytes=64, name="high%d" % turn)
+            nc.gpsimd.memset(low[:, PAIR_LEN - TAIL : PAIR_LEN], 0.0)
+            nc.gpsimd.memset(high[:].rearrange("p (r g) -> p r g", g=GROUP_ROWS)[:, :, GROUP_ROWS - TAIL : GROUP_ROWS], 0.0)
+            version_tiles.append((low, high))
 
         for n in range(n_groups + 2):
             if n + 3 < n_groups:

@@ -33,11 +33,15 @@ PASS_UNITS = 4
 PASSES = UNITS // PASS_UNITS
 STORE_ROWS = 8
 
-BANK_STRIPS = 2
+BANK_VALUES = 1024
 TURNED_BANKS = 3
 ACC_BANKS = PASSES
 VERSION_TILES = 3
 TAIL = 32
+
+
+def yield_of(chunks):
+    return chunks * P - (TAPS - 1)
 
 
 def plan_groups():
@@ -45,11 +49,13 @@ def plan_groups():
     end = ALL_ROWS - (TAPS - 1)
     start = 0
     while start < end:
-        stop = min(start + GROUP_ROWS - (TAPS - 1), end)
+        left = end - start
+        chunks = CHUNKS if left > yield_of(2) + yield_of(1) - STORE_ROWS else (2 if left > yield_of(1) else 1)
+        stop = min(start + yield_of(chunks), end)
         if stop < end:
             row = stop % SIDE_IN
             stop -= row % STORE_ROWS if row <= SIDE_OUT else row - SIDE_OUT
-        groups.append((min(start, ALL_ROWS - GROUP_ROWS), start, stop))
+        groups.append((min(start, ALL_ROWS - chunks * P), start, stop, chunks))
         start = stop + (TAPS - 1 if stop % SIDE_IN == SIDE_OUT else 0)
     return groups
 
@@ -75,10 +81,10 @@ def bias_on_partitions(nc, const, turn_psum, identity, bias):
     bias_square = const.tile([P, C_OUT], BF16)
     nc.vector.memset(bias_square[:], 0.0)
     nc.scalar.dma_start(out=bias_square[0:1, :], in_=bias.unsqueeze(0))
-    bias_turned = turn_psum.tile([P, BANK_STRIPS, CHUNKS, P], BF16, name="turned")
-    nc.tensor.transpose(bias_turned[:, 0, 0, :], bias_square[:], identity[:])
+    bias_turned = turn_psum.tile([P, BANK_VALUES], BF16, name="turned")
+    nc.tensor.transpose(bias_turned[:, 0:P], bias_square[:], identity[:])
     bias_column = const.tile([P, 1], F32)
-    nc.vector.tensor_copy(out=bias_column[:], in_=bias_turned[:, 0, 0, 0:1])
+    nc.vector.tensor_copy(out=bias_column[:], in_=bias_turned[:, 0:1])
     return bias_column
 
 
@@ -103,57 +109,72 @@ def tile_conv2d_kernel(tc, x, weights_words, weights_scales, bias, out):
         codes_of = {}
 
         def load_rows(n):
-            base = groups[n][0]
+            base, chunks = groups[n][0], groups[n][3]
             rows = rows_pool.tile([P, TAPS, CHUNKS, SIDE_OUT], BF16, name="rows")
             rows_of[n] = rows
             for e in range(2):
                 for pair in range(2):
                     first = 2 * pair + e
                     nc.sync.dma_start(
-                        out=rows[:, 2 * e + pair, :, :],
-                        in_=x_rows[base : base + GROUP_ROWS, first : first + SIDE_OUT].rearrange("(k p) w -> p k w", p=P),
+                        out=rows[:, 2 * e + pair, 0:chunks, :],
+                        in_=x_rows[base : base + chunks * P, first : first + SIDE_OUT].rearrange("(k p) w -> p k w", p=P),
                     )
 
         def build_windows(n):
+            chunks = groups[n][3]
             windows = window_pool.tile([P, CHUNKS, STRIPS * P], BF16, name="windows")
             windows_of[n] = windows
             nc.vector.tensor_copy(
-                out=windows[:].bitcast(F32).rearrange("p k (w f) -> p k w f", f=TAPS),
-                in_=rows_of[n][:].bitcast(F32).rearrange("p f k w -> p k w f"),
+                out=windows[:, 0:chunks, :].bitcast(F32).rearrange("p k (w f) -> p k w f", f=TAPS),
+                in_=rows_of[n][:, :, 0:chunks, :].bitcast(F32).rearrange("p f k w -> p k w f"),
             )
 
         def turn_and_seed(n):
             low, high = version_tiles[n % VERSION_TILES]
             versions_of[n] = (low, high)
             windows = windows_of[n]
-            for bank in range(TURNED_BANKS):
-                strips = range(bank * BANK_STRIPS, min((bank + 1) * BANK_STRIPS, STRIPS))
-                turned = turn_psum.tile([P, BANK_STRIPS, CHUNKS, P], BF16, name="turned")
+            chunks = groups[n][3]
+            run = chunks * P
+            bank_strips = BANK_VALUES // run
+            for first_strip in range(0, STRIPS, bank_strips):
+                strips = range(first_strip, min(first_strip + bank_strips, STRIPS))
+                turned = turn_psum.tile([P, BANK_VALUES], BF16, name="turned")
                 for strip in strips:
-                    for chunk in range(CHUNKS):
+                    for chunk in range(chunks):
+                        place = (strip - first_strip) * run + chunk * P
                         nc.tensor.transpose(
-                            turned[:, strip % BANK_STRIPS, chunk, :],
+                            turned[:, place : place + P],
                             windows[:, chunk, strip * P : (strip + 1) * P],
                             identity[:],
                         )
-                flat = turned[:].rearrange("p s k g -> p (s k g)")
-                first = bank * BANK_STRIPS * GROUP_ROWS
-                length = len(strips) * GROUP_ROWS
-                nc.scalar.copy(out=low[:, first : first + length], in_=flat[:, 0:length])
-                nc.scalar.copy(out=high[:, first : first + length - 2], in_=flat[:, 2:length])
+                first = first_strip * run
+                length = len(strips) * run
+                nc.scalar.copy(out=low[:, first : first + length], in_=turned[:, 0:length])
+                if strips[-1] < STRIPS - 1:
+                    nc.scalar.copy(out=high[:, first : first + length - 2], in_=turned[:, 2:length])
 
-        def odd_versions(n):
+        def version_one(n):
+            low = versions_of[n][0]
+            length = STRIPS * groups[n][3] * P
+            nc.vector.tensor_copy(out=low[:, length : 2 * length - 1], in_=low[:, 1:length])
+
+        def version_three(n):
             low, high = versions_of[n]
-            nc.vector.tensor_copy(out=low[:, VERSION_LEN : PAIR_LEN - 1], in_=low[:, 1:VERSION_LEN])
-            nc.vector.tensor_copy(out=high[:, VERSION_LEN : PAIR_LEN - 2], in_=low[:, VERSION_LEN + 2 : PAIR_LEN])
+            run = groups[n][3] * P
+            length = STRIPS * run
+            bank_strips = BANK_VALUES // run
+            left = (STRIPS - 1) // bank_strips * bank_strips * run
+            nc.vector.tensor_copy(out=high[:, left : 2 * length - 2], in_=low[:, left + 2 : 2 * length])
 
         def quantise(n):
             a_codes = code_pool.tile([P, UNITS * WORDS], U32, align_bytes=64, name="a_codes")
             a_scales = code_pool.tile([P, UNITS * WORDS], U8, align_bytes=64, name="a_scales")
             codes_of[n] = (a_codes, a_scales)
+            pair_len = 2 * STRIPS * groups[n][3] * P
+            cut = 4 * pair_len // 5
             for half, values in enumerate(versions_of[n]):
-                for first, last in ((0, 4096), (4096, PAIR_LEN)):
-                    words = slice((half * PAIR_LEN + first) // TAPS, (half * PAIR_LEN + last) // TAPS)
+                for first, last in ((0, cut), (cut, pair_len)):
+                    words = slice((half * pair_len + first) // TAPS, (half * pair_len + last) // TAPS)
                     nc.vector.quantize_mx(
                         out=a_codes[:, words].bitcast(FP8X4),
                         scales=a_scales[:, words],
@@ -162,15 +183,17 @@ def tile_conv2d_kernel(tc, x, weights_words, weights_scales, bias, out):
 
         def multiply_and_store(n):
             a_codes, a_scales = codes_of[n]
+            base, g, stop, chunks = groups[n]
+            words = chunks * P // TAPS
             result = result_pool.tile([P, WORDS * UNITS], F32, name="result")
-            result_by_unit = result[:].rearrange("o (j u) -> o j u", u=UNITS)
+            result_by_unit = result[:, 0 : words * UNITS].rearrange("o (j u) -> o j u", u=UNITS)
             accs = []
             for z in range(PASSES):
                 acc = acc_psum.tile([P, PASS_UNITS * WORDS], F32, name="acc")
                 accs.append(acc)
-                moving = slice(z * PASS_UNITS * WORDS, (z + 1) * PASS_UNITS * WORDS)
+                moving = slice(z * PASS_UNITS * words, (z + 1) * PASS_UNITS * words)
                 nc.tensor.matmul_mx(
-                    out=acc[:],
+                    out=acc[:, 0 : PASS_UNITS * words],
                     lhsT=w_swapped[:].bitcast(FP8X4),
                     lhsT_scale=w_scales[:],
                     rhs=a_codes[:, moving].bitcast(FP8X4),
@@ -181,11 +204,10 @@ def tile_conv2d_kernel(tc, x, weights_words, weights_scales, bias, out):
             for z in range(PASSES):
                 nc.scalar.activation(
                     out=result_by_unit[:, :, z * PASS_UNITS : (z + 1) * PASS_UNITS],
-                    in_=accs[z][:].rearrange("o (u j) -> o j u", u=PASS_UNITS),
+                    in_=accs[z][:, 0 : PASS_UNITS * words].rearrange("o (u j) -> o j u", u=PASS_UNITS),
                     func=mybir.ActivationFunctionType.Identity,
                     bias=bias_column[:, 0:1],
                 )
-            base, g, stop = groups[n]
             while g < stop:
                 image, row = divmod(g, SIDE_IN)
                 g_end = min(stop, image * SIDE_IN + SIDE_OUT)
@@ -231,12 +253,14 @@ def tile_conv2d_kernel(tc, x, weights_words, weights_scales, bias, out):
         for n in range(n_groups + 2):
             if n + 3 < n_groups:
                 load_rows(n + 3)
+            if 0 <= n - 1 < n_groups:
+                version_one(n - 1)
             if n + 1 < n_groups:
                 build_windows(n + 1)
             if n < n_groups:
                 turn_and_seed(n)
             if 0 <= n - 1 < n_groups:
-                odd_versions(n - 1)
+                version_three(n - 1)
                 quantise(n - 1)
             if 0 <= n - 2 < n_groups:
                 multiply_and_store(n - 2)

@@ -125,8 +125,8 @@ def tile_conv2d_kernel(tc, x, weights_words, weights_scales, bias, out):
             windows = window_pool.tile([P, CHUNKS, STRIPS * P], BF16, name="windows")
             windows_of[n] = windows
             nc.vector.tensor_copy(
-                out=windows[:, 0:chunks, :].bitcast(F32).rearrange("p k (w f) -> p k w f", f=TAPS),
-                in_=rows_of[n][:, :, 0:chunks, :].bitcast(F32).rearrange("p f k w -> p k w f"),
+                out=windows[:, 0:chunks, :].bitcast(F32).rearrange("p k (c i f) -> p (k c) f i", i=4, f=TAPS),
+                in_=rows_of[n][:, :, 0:chunks, :].bitcast(F32).rearrange("p f k (c i) -> p (k c) f i", i=4),
             )
 
         def turn_and_seed(n):

@@ -156,7 +156,7 @@ def tile_conv2d_kernel(tc, x, weights_words, weights_scales, bias, out):
         def version_one(n):
             low = versions_of[n][0]
             length = STRIPS * groups[n][3] * P
-            nc.vector.tensor_copy(out=low[:, length : 2 * length - 1], in_=low[:, 1:length])
+            nc.vector.tensor_copy(out=low[:, length : 2 * length - TAPS], in_=low[:, 1 : length - TAPS + 1])
 
         def version_three(n):
             low, high = versions_of[n]
@@ -164,7 +164,8 @@ def tile_conv2d_kernel(tc, x, weights_words, weights_scales, bias, out):
             length = STRIPS * run
             bank_strips = BANK_VALUES // run
             left = (STRIPS - 1) // bank_strips * bank_strips * run
-            nc.vector.tensor_copy(out=high[:, left : 2 * length - 2], in_=low[:, left + 2 : 2 * length])
+            nc.vector.tensor_copy(out=high[:, length : 2 * length - TAPS], in_=low[:, 3 : length - TAPS + 3])
+            nc.vector.tensor_copy(out=high[:, left : length - TAPS], in_=low[:, left + 2 : length - TAPS + 2])
 
         def quantise(n):
             a_codes = code_pool.tile([P, UNITS * WORDS], U32, align_bytes=64, name="a_codes")

@@ -77,15 +77,17 @@ def load_weight_scales(nc, w_scales, weights_scales):
         )
 
 
-def bias_on_partitions(nc, const, turn_psum, identity, bias):
+def load_bias(nc, const, bias):
     bias_square = const.tile([P, C_OUT], BF16)
     nc.vector.memset(bias_square[:], 0.0)
     nc.scalar.dma_start(out=bias_square[0:1, :], in_=bias.unsqueeze(0))
-    bias_turned = turn_psum.tile([P, BANK_VALUES], BF16, name="turned")
+    return bias_square
+
+
+def turn_bias(nc, acc_psum, identity, bias_square):
+    bias_turned = acc_psum.tile([P, BANK_VALUES], BF16, name="acc")
     nc.tensor.transpose(bias_turned[:, 0:P], bias_square[:], identity[:])
-    bias_column = const.tile([P, 1], F32)
-    nc.vector.tensor_copy(out=bias_column[:], in_=bias_turned[:, 0:1])
-    return bias_column
+    return bias_turned
 
 
 def tile_conv2d_kernel(tc, x, weights_words, weights_scales, bias, out):
@@ -221,27 +223,34 @@ def tile_conv2d_kernel(tc, x, weights_words, weights_scales, bias, out):
                 )
                 g = g_end + TAPS - 1
 
+        load_rows(0)
+        load_rows(1)
         identity = const.tile([P, P], BF16)
         make_identity(nc, identity[:])
         w_scales = const.tile([P, C_OUT], U8, align_bytes=64)
         nc.vector.memset(w_scales[:].bitcast(I32), 0)
+        bias_square = load_bias(nc, const, bias)
         w_codes = load_weight_codes(nc, const, weights_words)
-        load_rows(0)
+        load_rows(2)
         load_weight_scales(nc, w_scales, weights_scales)
-        bias_column = bias_on_partitions(nc, const, turn_psum, identity, bias)
+        build_windows(0)
         w_planes = const.tile([P, TAPS, C_OUT], U8, align_bytes=64)
         nc.vector.tensor_copy(out=w_planes[:], in_=w_codes[:].rearrange("p (n t) -> p t n", t=TAPS))
         w_moved = const.tile([P, TAPS, C_OUT], U8, align_bytes=64)
-        for di in range(TAPS):
-            for dj in range(TAPS):
-                nc.sync.dma_start(out=w_moved[dj:P:TAPS, di, :].bitcast(I32), in_=w_planes[di:P:TAPS, dj, :].bitcast(I32))
-        load_rows(1)
-        load_rows(2)
-        build_windows(0)
         w_swapped = const.tile([P, TAPS * C_OUT], U8, align_bytes=64)
-        nc.vector.tensor_copy(
-            out=w_swapped[:].rearrange("p (n t) -> p n t", t=TAPS), in_=w_moved[:].rearrange("p t n -> p n t")
-        )
+        bias_column = const.tile([P, 1], F32)
+
+        def move_weight_codes():
+            for di in range(TAPS):
+                for dj in range(TAPS):
+                    nc.sync.dma_start(
+                        out=w_moved[dj:P:TAPS, di, :].bitcast(I32), in_=w_planes[di:P:TAPS, dj, :].bitcast(I32)
+                    )
+
+        def weave_weight_codes():
+            nc.vector.tensor_copy(
+                out=w_swapped[:].rearrange("p (n t) -> p n t", t=TAPS), in_=w_moved[:].rearrange("p t n -> p n t")
+            )
 
         version_tiles = []
         for turn in range(VERSION_TILES):
@@ -254,14 +263,21 @@ def tile_conv2d_kernel(tc, x, weights_words, weights_scales, bias, out):
         for n in range(n_groups + 2):
             if n + 3 < n_groups:
                 load_rows(n + 3)
+            if n == 0:
+                move_weight_codes()
             if 0 <= n - 1 < n_groups:
                 version_one(n - 1)
             if n + 1 < n_groups:
                 build_windows(n + 1)
             if n < n_groups:
                 turn_and_seed(n)
+            if n == 0:
+                bias_turned = turn_bias(nc, acc_psum, identity, bias_square)
             if 0 <= n - 1 < n_groups:
                 version_three(n - 1)
                 quantise(n - 1)
+            if n == 1:
+                nc.vector.tensor_copy(out=bias_column[:], in_=bias_turned[:, 0:1])
+                weave_weight_codes()
             if 0 <= n - 2 < n_groups:
                 multiply_and_store(n - 2)

@@ -33,6 +33,11 @@ PASS_UNITS = 4
 PASSES = UNITS // PASS_UNITS
 STORE_ROWS = 8
 
+ROW_LEN = SIDE_IN - 1
+ROW_PITCH = 176
+WINDOW_START = 8
+WINDOW_PITCH = 672
+
 BANK_VALUES = 1024
 TURNED_BANKS = 3
 ACC_BANKS = PASSES
@@ -112,23 +117,29 @@ def tile_conv2d_kernel(tc, x, weights_words, weights_scales, bias, out):
 
         def load_rows(n):
             base, chunks = groups[n][0], groups[n][3]
-            rows = rows_pool.tile([P, TAPS, CHUNKS, SIDE_OUT], BF16, name="rows")
+            rows = rows_pool.tile([P, 2, CHUNKS, ROW_PITCH], BF16, name="rows")
             rows_of[n] = rows
             for e in range(2):
-                for pair in range(2):
-                    first = 2 * pair + e
-                    nc.sync.dma_start(
-                        out=rows[:, 2 * e + pair, 0:chunks, :],
-                        in_=x_rows[base : base + chunks * P, first : first + SIDE_OUT].rearrange("(k p) w -> p k w", p=P),
-                    )
+                nc.sync.dma_start(
+                    out=rows[:, e, 0:chunks, 0:ROW_LEN],
+                    in_=x_rows[base : base + chunks * P, e : e + ROW_LEN].rearrange("(k p) w -> p k w", p=P),
+                )
 
         def build_windows(n):
             chunks = groups[n][3]
-            windows = window_pool.tile([P, CHUNKS, STRIPS * P], BF16, name="windows")
+            windows = window_pool.tile([P, CHUNKS, WINDOW_PITCH], BF16, align_bytes=64, name="windows")
             windows_of[n] = windows
+            words = ROW_LEN // 2
+            first = WINDOW_START // 2 - 2
             nc.vector.tensor_copy(
-                out=windows[:, 0:chunks, :].bitcast(F32).rearrange("p k (c i f) -> p (k c) f i", i=4, f=TAPS),
-                in_=rows_of[n][:, :, 0:chunks, :].bitcast(F32).rearrange("p f k (c i) -> p (k c) f i", i=4),
+                out=windows[:].bitcast(F32)[:, 0:chunks, first : first + 4 * words].rearrange(
+                    "p k (h r e) -> p k h r e", r=2, e=2
+                ),
+                in_=rows_of[n][:]
+                .bitcast(F32)[:, :, 0:chunks, 0:words]
+                .rearrange("p e k h -> p k h e")
+                .unsqueeze(3)
+                .to_broadcast([P, chunks, words, 2, 2]),
             )
 
         def turn_and_seed(n):
@@ -146,7 +157,7 @@ def tile_conv2d_kernel(tc, x, weights_words, weights_scales, bias, out):
                         place = (strip - first_strip) * run + chunk * P
                         nc.tensor.transpose(
                             turned[:, place : place + P],
-                            windows[:, chunk, strip * P : (strip + 1) * P],
+                            windows[:, chunk, WINDOW_START + strip * P : WINDOW_START + (strip + 1) * P],
                             identity[:],
                         )
                 first = first_strip * run
@@ -243,9 +254,11 @@ def tile_conv2d_kernel(tc, x, weights_words, weights_scales, bias, out):
         def move_weight_codes():
             for di in range(TAPS):
                 for dj in range(TAPS):
-                    nc.sync.dma_start(
-                        out=w_moved[dj:P:TAPS, di, :].bitcast(I32), in_=w_planes[di:P:TAPS, dj, :].bitcast(I32)
-                    )
+                    for e in range(2):
+                        place = 4 * (dj // 2) + 2 * e + dj % 2
+                        nc.sync.dma_start(
+                            out=w_moved[place:P:8, di, :].bitcast(I32), in_=w_planes[4 * e + di : P : 8, dj, :].bitcast(I32)
+                        )
 
         def weave_weight_codes():
             nc.vector.tensor_copy(

@@ -119,11 +119,14 @@ def tile_conv2d_kernel(tc, x, weights_words, weights_scales, bias, out):
             base, chunks = groups[n][0], groups[n][3]
             rows = rows_pool.tile([P, 2, CHUNKS, ROW_PITCH], BF16, name="rows")
             rows_of[n] = rows
-            for e in range(2):
-                nc.sync.dma_start(
-                    out=rows[:, e, 0:chunks, 0:ROW_LEN],
-                    in_=x_rows[base : base + chunks * P, e : e + ROW_LEN].rearrange("(k p) w -> p k w", p=P),
-                )
+            nc.sync.dma_start(
+                out=rows[:, 0, 0:chunks, 0:SIDE_IN],
+                in_=x_rows[base : base + chunks * P, :].rearrange("(k p) w -> p k w", p=P),
+            )
+
+        def shift_rows(n):
+            rows, chunks = rows_of[n], groups[n][3]
+            nc.scalar.copy(out=rows[:, 1, 0:chunks, 0:ROW_LEN], in_=rows[:, 0, 0:chunks, 1:SIDE_IN])
 
         def build_windows(n):
             chunks = groups[n][3]
@@ -148,6 +151,7 @@ def tile_conv2d_kernel(tc, x, weights_words, weights_scales, bias, out):
             windows = windows_of[n]
             chunks = groups[n][3]
             run = chunks * P
+            length = STRIPS * run
             bank_strips = BANK_VALUES // run
             for first_strip in range(0, STRIPS, bank_strips):
                 strips = range(first_strip, min(first_strip + bank_strips, STRIPS))
@@ -161,10 +165,9 @@ def tile_conv2d_kernel(tc, x, weights_words, weights_scales, bias, out):
                             identity[:],
                         )
                 first = first_strip * run
-                length = len(strips) * run
-                nc.scalar.copy(out=low[:, first : first + length], in_=turned[:, 0:length])
-                if strips[-1] < STRIPS - 1:
-                    nc.scalar.copy(out=high[:, first : first + length - 2], in_=turned[:, 2:length])
+                filled = len(strips) * run
+                nc.scalar.copy(out=low[:, first : first + filled], in_=turned[:, 0:filled])
+            nc.sync.dma_start(out=high[:, 0 : length - TAPS], in_=low[:, 2 : length - TAPS + 2])
 
         def version_one(n):
             low = versions_of[n][0]
@@ -173,12 +176,8 @@ def tile_conv2d_kernel(tc, x, weights_words, weights_scales, bias, out):
 
         def version_three(n):
             low, high = versions_of[n]
-            run = groups[n][3] * P
-            length = STRIPS * run
-            bank_strips = BANK_VALUES // run
-            left = (STRIPS - 1) // bank_strips * bank_strips * run
+            length = STRIPS * groups[n][3] * P
             nc.vector.tensor_copy(out=high[:, length : 2 * length - TAPS], in_=low[:, 3 : length - TAPS + 3])
-            nc.vector.tensor_copy(out=high[:, left : length - TAPS], in_=low[:, left + 2 : length - TAPS + 2])
 
         def quantise(n):
             a_codes = code_pool.tile([P, UNITS * WORDS], U32, align_bytes=64, name="a_codes")
@@ -244,6 +243,8 @@ def tile_conv2d_kernel(tc, x, weights_words, weights_scales, bias, out):
         w_codes = load_weight_codes(nc, const, weights_words)
         load_rows(2)
         load_weight_scales(nc, w_scales, weights_scales)
+        shift_rows(0)
+        shift_rows(1)
         build_windows(0)
         w_planes = const.tile([P, TAPS, C_OUT], U8, align_bytes=64)
         nc.vector.tensor_copy(out=w_planes[:], in_=w_codes[:].rearrange("p (n t) -> p t n", t=TAPS))
@@ -284,6 +285,8 @@ def tile_conv2d_kernel(tc, x, weights_words, weights_scales, bias, out):
                 build_windows(n + 1)
             if n < n_groups:
                 turn_and_seed(n)
+            if n + 2 < n_groups:
+                shift_rows(n + 2)
             if n == 0:
                 bias_turned = turn_bias(nc, acc_psum, identity, bias_square)
             if 0 <= n - 1 < n_groups:

@@ -179,20 +179,22 @@ def tile_conv2d_kernel(tc, x, weights_words, weights_scales, bias, out):
             length = STRIPS * groups[n][3] * P
             nc.vector.tensor_copy(out=high[:, length : 2 * length - TAPS], in_=low[:, 3 : length - TAPS + 3])
 
-        def quantise(n):
-            a_codes = code_pool.tile([P, UNITS * WORDS], U32, align_bytes=64, name="a_codes")
-            a_scales = code_pool.tile([P, UNITS * WORDS], U8, align_bytes=64, name="a_scales")
-            codes_of[n] = (a_codes, a_scales)
+        def quantise(n, half):
+            if half == 0:
+                a_codes = code_pool.tile([P, UNITS * WORDS], U32, align_bytes=64, name="a_codes")
+                a_scales = code_pool.tile([P, UNITS * WORDS], U8, align_bytes=64, name="a_scales")
+                codes_of[n] = (a_codes, a_scales)
+            a_codes, a_scales = codes_of[n]
+            values = versions_of[n][half]
             pair_len = 2 * STRIPS * groups[n][3] * P
             cut = 4 * pair_len // 5
-            for half, values in enumerate(versions_of[n]):
-                for first, last in ((0, cut), (cut, pair_len)):
-                    words = slice((half * pair_len + first) // TAPS, (half * pair_len + last) // TAPS)
-                    nc.vector.quantize_mx(
-                        out=a_codes[:, words].bitcast(FP8X4),
-                        scales=a_scales[:, words],
-                        in_=values[:, first:last],
-                    )
+            for first, last in ((0, cut), (cut, pair_len)):
+                words = slice((half * pair_len + first) // TAPS, (half * pair_len + last) // TAPS)
+                nc.vector.quantize_mx(
+                    out=a_codes[:, words].bitcast(FP8X4),
+                    scales=a_scales[:, words],
+                    in_=values[:, first:last],
+                )
 
         def multiply_and_store(n):
             a_codes, a_scales = codes_of[n]
@@ -279,6 +281,8 @@ def tile_conv2d_kernel(tc, x, weights_words, weights_scales, bias, out):
                 load_rows(n + 3)
             if n == 0:
                 move_weight_codes()
+            if 0 <= n - 2 < n_groups:
+                quantise(n - 2, 1)
             if 0 <= n - 1 < n_groups:
                 version_one(n - 1)
             if n + 1 < n_groups:
@@ -291,7 +295,7 @@ def tile_conv2d_kernel(tc, x, weights_words, weights_scales, bias, out):
                 bias_turned = turn_bias(nc, acc_psum, identity, bias_square)
             if 0 <= n - 1 < n_groups:
                 version_three(n - 1)
-                quantise(n - 1)
+                quantise(n - 1, 0)
             if n == 1:
                 nc.vector.tensor_copy(out=bias_column[:], in_=bias_turned[:, 0:1])
                 weave_weight_codes()

@@ -41,6 +41,7 @@ WINDOW_PITCH = 672
 BANK_VALUES = 1024
 TURNED_BANKS = 3
 ACC_BANKS = PASSES
+LEAD_CHUNKS = (1, 1, 2)
 VERSION_TILES = 3
 TAIL = 32
 
@@ -55,7 +56,10 @@ def plan_groups():
     start = 0
     while start < end:
         left = end - start
-        chunks = CHUNKS if left > yield_of(2) + yield_of(1) - STORE_ROWS else (2 if left > yield_of(1) else 1)
+        if len(groups) < len(LEAD_CHUNKS):
+            chunks = LEAD_CHUNKS[len(groups)]
+        else:
+            chunks = CHUNKS if left > yield_of(2) + yield_of(1) - STORE_ROWS else (2 if left > yield_of(1) else 1)
         stop = min(start + yield_of(chunks), end)
         if stop < end:
             row = stop % SIDE_IN
@@ -102,9 +106,9 @@ def tile_conv2d_kernel(tc, x, weights_words, weights_scales, bias, out):
     x_rows = x.rearrange("b c h w -> (b c h) w")
     with ExitStack() as ctx:
         const = ctx.enter_context(tc.tile_pool(name="const", bufs=1))
-        rows_pool = ctx.enter_context(tc.tile_pool(name="rows", bufs=4))
+        rows_pool = ctx.enter_context(tc.tile_pool(name="rows", bufs=5))
         window_pool = ctx.enter_context(tc.tile_pool(name="windows", bufs=2))
-        code_pool = ctx.enter_context(tc.tile_pool(name="codes", bufs=3))
+        code_pool = ctx.enter_context(tc.tile_pool(name="codes", bufs=4))
         result_pool = ctx.enter_context(tc.tile_pool(name="result", bufs=3))
         turn_psum = ctx.enter_context(tc.psum_pool(name="turned", bufs=TURNED_BANKS))
         acc_psum = ctx.enter_context(tc.psum_pool(name="acc", bufs=ACC_BANKS))
@@ -167,7 +171,15 @@ def tile_conv2d_kernel(tc, x, weights_words, weights_scales, bias, out):
                 first = first_strip * run
                 filled = len(strips) * run
                 nc.scalar.copy(out=low[:, first : first + filled], in_=turned[:, 0:filled])
-            nc.sync.dma_start(out=high[:, 0 : length - TAPS], in_=low[:, 2 : length - TAPS + 2])
+                if chunks < CHUNKS:
+                    nc.scalar.copy(out=high[:, first : first + filled - TAPS], in_=turned[:, 2 : filled - TAPS + 2])
+                if first_strip == 0:
+                    third = length + first
+                    nc.scalar.copy(out=high[:, third : third + filled - TAPS], in_=turned[:, 3 : filled - TAPS + 3])
+            if chunks == CHUNKS:
+                nc.sync.dma_start(
+                    out=high[:, 0 : length - TAPS], in_=low[:, 2 : length - TAPS + 2]
+                )
 
         def version_one(n):
             low = versions_of[n][0]
@@ -176,8 +188,13 @@ def tile_conv2d_kernel(tc, x, weights_words, weights_scales, bias, out):
 
         def version_three(n):
             low, high = versions_of[n]
-            length = STRIPS * groups[n][3] * P
-            nc.vector.tensor_copy(out=high[:, length : 2 * length - TAPS], in_=low[:, 3 : length - TAPS + 3])
+            run = groups[n][3] * P
+            length = STRIPS * run
+            done = BANK_VALUES // run * run
+            if done < length:
+                nc.vector.tensor_copy(
+                    out=high[:, length + done : 2 * length - TAPS], in_=low[:, done + 3 : length - TAPS + 3]
+                )
 
         def quantise(n, half):
             if half == 0:
@@ -236,20 +253,21 @@ def tile_conv2d_kernel(tc, x, weights_words, weights_scales, bias, out):
                 g = g_end + TAPS - 1
 
         load_rows(0)
+        w_codes = load_weight_codes(nc, const, weights_words)
         load_rows(1)
+        load_rows(2)
         identity = const.tile([P, P], BF16)
         make_identity(nc, identity[:])
         w_scales = const.tile([P, C_OUT], U8, align_bytes=64)
         nc.vector.memset(w_scales[:].bitcast(I32), 0)
         bias_square = load_bias(nc, const, bias)
-        w_codes = load_weight_codes(nc, const, weights_words)
-        load_rows(2)
+        load_rows(3)
         load_weight_scales(nc, w_scales, weights_scales)
+        w_planes = const.tile([P, TAPS, C_OUT], U8, align_bytes=64)
+        nc.vector.tensor_copy(out=w_planes[:], in_=w_codes[:].rearrange("p (n t) -> p t n", t=TAPS))
         shift_rows(0)
         shift_rows(1)
         build_windows(0)
-        w_planes = const.tile([P, TAPS, C_OUT], U8, align_bytes=64)
-        nc.vector.tensor_copy(out=w_planes[:], in_=w_codes[:].rearrange("p (n t) -> p t n", t=TAPS))
         w_moved = const.tile([P, TAPS, C_OUT], U8, align_bytes=64)
         w_swapped = const.tile([P, TAPS * C_OUT], U8, align_bytes=64)
         bias_column = const.tile([P, 1], F32)
@@ -264,7 +282,7 @@ def tile_conv2d_kernel(tc, x, weights_words, weights_scales, bias, out):
                         )
 
         def weave_weight_codes():
-            nc.vector.tensor_copy(
+            nc.gpsimd.tensor_copy(
                 out=w_swapped[:].rearrange("p (n t) -> p n t", t=TAPS), in_=w_moved[:].rearrange("p t n -> p n t")
             )
 
@@ -274,13 +292,18 @@ def tile_conv2d_kernel(tc, x, weights_words, weights_scales, bias, out):
             high = const.tile([P, PAIR_LEN], BF16, align_bytes=64, name="high%d" % turn)
             nc.gpsimd.memset(low[:, PAIR_LEN - TAIL : PAIR_LEN], 0.0)
             nc.gpsimd.memset(high[:].rearrange("p (r g) -> p r g", g=GROUP_ROWS)[:, :, GROUP_ROWS - TAIL : GROUP_ROWS], 0.0)
+            run = groups[turn][3] * P
+            pair_len = 2 * STRIPS * run
+            nc.gpsimd.memset(low[:, pair_len - TAIL : pair_len], 0.0)
+            nc.gpsimd.memset(high[:, 0:pair_len].rearrange("p (r g) -> p r g", g=run)[:, :, run - TAIL : run], 0.0)
             version_tiles.append((low, high))
 
         for n in range(n_groups + 2):
-            if n + 3 < n_groups:
-                load_rows(n + 3)
+            if n + 4 < n_groups:
+                load_rows(n + 4)
             if n == 0:
                 move_weight_codes()
+                weave_weight_codes()
             if 0 <= n - 2 < n_groups:
                 quantise(n - 2, 1)
             if 0 <= n - 1 < n_groups:
@@ -298,6 +321,5 @@ def tile_conv2d_kernel(tc, x, weights_words, weights_scales, bias, out):
                 quantise(n - 1, 0)
             if n == 1:
                 nc.vector.tensor_copy(out=bias_column[:], in_=bias_turned[:, 0:1])
-                weave_weight_codes()
             if 0 <= n - 2 < n_groups:
                 multiply_and_store(n - 2)

@@ -173,7 +173,7 @@ def tile_conv2d_kernel(tc, x, weights_words, weights_scales, bias, out):
                 nc.scalar.copy(out=low[:, first : first + filled], in_=turned[:, 0:filled])
                 if chunks < CHUNKS:
                     nc.scalar.copy(out=high[:, first : first + filled - TAPS], in_=turned[:, 2 : filled - TAPS + 2])
-                if first_strip == 0:
+                if strips[-1] == STRIPS - 1:
                     third = length + first
                     nc.scalar.copy(out=high[:, third : third + filled - TAPS], in_=turned[:, 3 : filled - TAPS + 3])
             if chunks == CHUNKS:
@@ -190,10 +190,11 @@ def tile_conv2d_kernel(tc, x, weights_words, weights_scales, bias, out):
             low, high = versions_of[n]
             run = groups[n][3] * P
             length = STRIPS * run
-            done = BANK_VALUES // run * run
-            if done < length:
+            bank_strips = BANK_VALUES // run
+            left = (STRIPS - 1) // bank_strips * bank_strips * run
+            if left > 0:
                 nc.vector.tensor_copy(
-                    out=high[:, length + done : 2 * length - TAPS], in_=low[:, done + 3 : length - TAPS + 3]
+                    out=high[:, length : length + left - TAPS], in_=low[:, 3 : left - TAPS + 3]
                 )
 
         def quantise(n, half):

@@ -41,8 +41,13 @@ WINDOW_PITCH = 672
 BANK_VALUES = 1024
 TURNED_BANKS = 3
 ACC_BANKS = PASSES
-LEAD_CHUNKS = (1, 1, 2)
-VERSION_TILES = 3
+LEAD_CHUNKS = (1,)
+GROUPS = 2
+BLOCKS = GROUPS * CHUNKS
+QUANTISE_WIDTHS = (4096, 2048, 1024, 512, 256, 128)
+LEAD_SETS = 4
+VECTOR_STRIPS = 4
+VERSION_TILES = 2
 TAIL = 32
 
 
@@ -67,6 +72,22 @@ def plan_groups():
         groups.append((min(start, ALL_ROWS - chunks * P), start, stop, chunks))
         start = stop + (TAPS - 1 if stop % SIDE_IN == SIDE_OUT else 0)
     return groups
+
+
+def plan_sets(groups):
+    full = [group for group in groups if group[3] == CHUNKS]
+    pairs = (len(full) - 2) // GROUPS
+    alone = len(full) - GROUPS * pairs
+    sets = [[group] for group in groups[: len(LEAD_CHUNKS)]]
+    sets.append([full[0]])
+    sets += [full[1 + GROUPS * k : 1 + GROUPS * (k + 1)] for k in range(pairs)]
+    sets += [[group] for group in full[len(full) - alone + 1 :]]
+    sets += [[group] for group in groups[len(LEAD_CHUNKS) + len(full) :]]
+    return sets
+
+
+def blocks_of(groups):
+    return sum(group[3] for group in groups)
 
 
 def load_weight_codes(nc, const, weights_words):
@@ -102,13 +123,14 @@ def turn_bias(nc, acc_psum, identity, bias_square):
 def tile_conv2d_kernel(tc, x, weights_words, weights_scales, bias, out):
     nc = tc.nc
     groups = plan_groups()
-    n_groups = len(groups)
+    sets = plan_sets(groups)
+    n_sets = len(sets)
     x_rows = x.rearrange("b c h w -> (b c h) w")
     with ExitStack() as ctx:
         const = ctx.enter_context(tc.tile_pool(name="const", bufs=1))
-        rows_pool = ctx.enter_context(tc.tile_pool(name="rows", bufs=5))
+        rows_pool = ctx.enter_context(tc.tile_pool(name="rows", bufs=3))
         window_pool = ctx.enter_context(tc.tile_pool(name="windows", bufs=2))
-        code_pool = ctx.enter_context(tc.tile_pool(name="codes", bufs=4))
+        code_pool = ctx.enter_context(tc.tile_pool(name="codes", bufs=2))
         result_pool = ctx.enter_context(tc.tile_pool(name="result", bufs=3))
         turn_psum = ctx.enter_context(tc.psum_pool(name="turned", bufs=TURNED_BANKS))
         acc_psum = ctx.enter_context(tc.psum_pool(name="acc", bufs=ACC_BANKS))
@@ -116,107 +138,116 @@ def tile_conv2d_kernel(tc, x, weights_words, weights_scales, bias, out):
 
         rows_of = {}
         windows_of = {}
-        versions_of = {}
         codes_of = {}
 
         def load_rows(n):
-            base, chunks = groups[n][0], groups[n][3]
-            rows = rows_pool.tile([P, 2, CHUNKS, ROW_PITCH], BF16, name="rows")
+            rows = rows_pool.tile([P, 2, BLOCKS, ROW_PITCH], BF16, name="rows")
             rows_of[n] = rows
-            nc.sync.dma_start(
-                out=rows[:, 0, 0:chunks, 0:SIDE_IN],
-                in_=x_rows[base : base + chunks * P, :].rearrange("(k p) w -> p k w", p=P),
-            )
+            for i, (base, first_row, stop, chunks) in enumerate(sets[n]):
+                nc.sync.dma_start(
+                    out=rows[:, 0, i * chunks : (i + 1) * chunks, 0:SIDE_IN],
+                    in_=x_rows[base : base + chunks * P, :].rearrange("(k p) w -> p k w", p=P),
+                )
 
         def shift_rows(n):
-            rows, chunks = rows_of[n], groups[n][3]
-            nc.scalar.copy(out=rows[:, 1, 0:chunks, 0:ROW_LEN], in_=rows[:, 0, 0:chunks, 1:SIDE_IN])
+            rows, blocks = rows_of[n], blocks_of(sets[n])
+            nc.scalar.copy(out=rows[:, 1, 0:blocks, 0:ROW_LEN], in_=rows[:, 0, 0:blocks, 1:SIDE_IN])
 
         def build_windows(n):
-            chunks = groups[n][3]
-            windows = window_pool.tile([P, CHUNKS, WINDOW_PITCH], BF16, align_bytes=64, name="windows")
+            blocks = blocks_of(sets[n])
+            windows = window_pool.tile([P, BLOCKS, WINDOW_PITCH], BF16, align_bytes=64, name="windows")
             windows_of[n] = windows
             words = ROW_LEN // 2
             first = WINDOW_START // 2 - 2
             nc.vector.tensor_copy(
-                out=windows[:].bitcast(F32)[:, 0:chunks, first : first + 4 * words].rearrange(
+                out=windows[:].bitcast(F32)[:, 0:blocks, first : first + 4 * words].rearrange(
                     "p k (h r e) -> p k h r e", r=2, e=2
                 ),
                 in_=rows_of[n][:]
-                .bitcast(F32)[:, :, 0:chunks, 0:words]
+                .bitcast(F32)[:, :, 0:blocks, 0:words]
                 .rearrange("p e k h -> p k h e")
                 .unsqueeze(3)
-                .to_broadcast([P, chunks, words, 2, 2]),
+                .to_broadcast([P, blocks, words, 2, 2]),
             )
 
+        def by_group(n):
+            length = STRIPS * sets[n][0][3] * P
+            versions = version_tiles[n % VERSION_TILES][:, 0 : len(sets[n]) * VERSIONS * length]
+            return versions.rearrange("p (i x) -> p i x", x=VERSIONS * length), length
+
         def turn_and_seed(n):
-            low, high = version_tiles[n % VERSION_TILES]
-            versions_of[n] = (low, high)
             windows = windows_of[n]
-            chunks = groups[n][3]
+            chunks = sets[n][0][3]
             run = chunks * P
-            length = STRIPS * run
+            versions, length = by_group(n)
+            runs = version_tiles[n % VERSION_TILES][:, 0 : len(sets[n]) * VERSIONS * length].rearrange(
+                "p (u g) -> p u g", g=run
+            )
+            strips = [(i, strip) for i in range(len(sets[n])) for strip in range(STRIPS)]
             bank_strips = BANK_VALUES // run
-            for first_strip in range(0, STRIPS, bank_strips):
-                strips = range(first_strip, min(first_strip + bank_strips, STRIPS))
+            for first in range(0, len(strips), bank_strips):
+                here = strips[first : first + bank_strips]
                 turned = turn_psum.tile([P, BANK_VALUES], BF16, name="turned")
-                for strip in strips:
+                for place, (i, strip) in enumerate(here):
                     for chunk in range(chunks):
-                        place = (strip - first_strip) * run + chunk * P
+                        at = place * run + chunk * P
                         nc.tensor.transpose(
-                            turned[:, place : place + P],
-                            windows[:, chunk, WINDOW_START + strip * P : WINDOW_START + (strip + 1) * P],
+                            turned[:, at : at + P],
+                            windows[:, i * chunks + chunk, WINDOW_START + strip * P : WINDOW_START + (strip + 1) * P],
                             identity[:],
                         )
-                first = first_strip * run
-                filled = len(strips) * run
-                nc.scalar.copy(out=low[:, first : first + filled], in_=turned[:, 0:filled])
-                if chunks < CHUNKS:
-                    nc.scalar.copy(out=high[:, first : first + filled - TAPS], in_=turned[:, 2 : filled - TAPS + 2])
-                if strips[-1] == STRIPS - 1:
-                    third = length + first
-                    nc.scalar.copy(out=high[:, third : third + filled - TAPS], in_=turned[:, 3 : filled - TAPS + 3])
+                places = [i * VERSIONS * STRIPS + strip for i, strip in here]
+                step = places[-1] - places[0] if len(here) == 2 else 1
+                nc.scalar.copy(
+                    out=runs[:, places[0] : places[-1] + 1 : step, :],
+                    in_=turned[:, 0 : len(here) * run].rearrange("p (u g) -> p u g", g=run),
+                )
             if chunks == CHUNKS:
                 nc.sync.dma_start(
-                    out=high[:, 0 : length - TAPS], in_=low[:, 2 : length - TAPS + 2]
+                    out=versions[:, :, 2 * length : 3 * length - TAPS], in_=versions[:, :, 2 : length - TAPS + 2]
                 )
+            else:
+                nc.scalar.copy(out=versions[:, :, 2 * length : 3 * length - TAPS], in_=versions[:, :, 2 : length - TAPS + 2])
+            share = VECTOR_STRIPS * run
+            nc.scalar.copy(
+                out=versions[:, :, 3 * length + share : 4 * length - TAPS], in_=versions[:, :, share + 3 : length - TAPS + 3]
+            )
 
         def version_one(n):
-            low = versions_of[n][0]
-            length = STRIPS * groups[n][3] * P
-            nc.vector.tensor_copy(out=low[:, length : 2 * length - TAPS], in_=low[:, 1 : length - TAPS + 1])
+            versions, length = by_group(n)
+            nc.vector.tensor_copy(out=versions[:, :, length : 2 * length - TAPS], in_=versions[:, :, 1 : length - TAPS + 1])
 
         def version_three(n):
-            low, high = versions_of[n]
-            run = groups[n][3] * P
-            length = STRIPS * run
-            bank_strips = BANK_VALUES // run
-            left = (STRIPS - 1) // bank_strips * bank_strips * run
-            if left > 0:
-                nc.vector.tensor_copy(
-                    out=high[:, length : length + left - TAPS], in_=low[:, 3 : left - TAPS + 3]
-                )
+            versions, length = by_group(n)
+            share = VECTOR_STRIPS * sets[n][0][3] * P
+            nc.vector.tensor_copy(
+                out=versions[:, :, 3 * length : 3 * length + share - TAPS], in_=versions[:, :, 3 : share - TAPS + 3]
+            )
 
-        def quantise(n, half):
-            if half == 0:
-                a_codes = code_pool.tile([P, UNITS * WORDS], U32, align_bytes=64, name="a_codes")
-                a_scales = code_pool.tile([P, UNITS * WORDS], U8, align_bytes=64, name="a_scales")
-                codes_of[n] = (a_codes, a_scales)
-            a_codes, a_scales = codes_of[n]
-            values = versions_of[n][half]
-            pair_len = 2 * STRIPS * groups[n][3] * P
-            cut = 4 * pair_len // 5
-            for first, last in ((0, cut), (cut, pair_len)):
-                words = slice((half * pair_len + first) // TAPS, (half * pair_len + last) // TAPS)
+        def quantise(n):
+            a_codes = code_pool.tile([P, GROUPS * UNITS * WORDS], U32, align_bytes=64, name="a_codes")
+            a_scales = code_pool.tile([P, GROUPS * UNITS * WORDS], U8, align_bytes=64, name="a_scales")
+            codes_of[n] = (a_codes, a_scales)
+            values = version_tiles[n % VERSION_TILES]
+            total = blocks_of(sets[n]) * P * UNITS
+            first = 0
+            while first < total:
+                last = first + max(width for width in QUANTISE_WIDTHS if width <= total - first)
+                words = slice(first // TAPS, last // TAPS)
                 nc.vector.quantize_mx(
                     out=a_codes[:, words].bitcast(FP8X4),
                     scales=a_scales[:, words],
                     in_=values[:, first:last],
                 )
+                first = last
 
         def multiply_and_store(n):
+            for i in range(len(sets[n])):
+                multiply_and_store_group(n, i)
+
+        def multiply_and_store_group(n, i):
             a_codes, a_scales = codes_of[n]
-            base, g, stop, chunks = groups[n]
+            base, g, stop, chunks = sets[n][i]
             words = chunks * P // TAPS
             result = result_pool.tile([P, WORDS * UNITS], F32, name="result")
             result_by_unit = result[:, 0 : words * UNITS].rearrange("o (j u) -> o j u", u=UNITS)
@@ -224,7 +255,7 @@ def tile_conv2d_kernel(tc, x, weights_words, weights_scales, bias, out):
             for z in range(PASSES):
                 acc = acc_psum.tile([P, PASS_UNITS * WORDS], F32, name="acc")
                 accs.append(acc)
-                moving = slice(z * PASS_UNITS * words, (z + 1) * PASS_UNITS * words)
+                moving = slice((i * UNITS + z * PASS_UNITS) * words, (i * UNITS + (z + 1) * PASS_UNITS) * words)
                 nc.tensor.matmul_mx(
                     out=acc[:, 0 : PASS_UNITS * words],
                     lhsT=w_swapped[:].bitcast(FP8X4),
@@ -262,7 +293,6 @@ def tile_conv2d_kernel(tc, x, weights_words, weights_scales, bias, out):
         w_scales = const.tile([P, C_OUT], U8, align_bytes=64)
         nc.vector.memset(w_scales[:].bitcast(I32), 0)
         bias_square = load_bias(nc, const, bias)
-        load_rows(3)
         load_weight_scales(nc, w_scales, weights_scales)
         w_planes = const.tile([P, TAPS, C_OUT], U8, align_bytes=64)
         nc.vector.tensor_copy(out=w_planes[:], in_=w_codes[:].rearrange("p (n t) -> p t n", t=TAPS))
@@ -289,38 +319,35 @@ def tile_conv2d_kernel(tc, x, weights_words, weights_scales, bias, out):
 
         version_tiles = []
         for turn in range(VERSION_TILES):
-            low = const.tile([P, PAIR_LEN], BF16, align_bytes=64, name="low%d" % turn)
-            high = const.tile([P, PAIR_LEN], BF16, align_bytes=64, name="high%d" % turn)
-            nc.gpsimd.memset(low[:, PAIR_LEN - TAIL : PAIR_LEN], 0.0)
-            nc.gpsimd.memset(high[:].rearrange("p (r g) -> p r g", g=GROUP_ROWS)[:, :, GROUP_ROWS - TAIL : GROUP_ROWS], 0.0)
-            run = groups[turn][3] * P
-            pair_len = 2 * STRIPS * run
-            nc.gpsimd.memset(low[:, pair_len - TAIL : pair_len], 0.0)
-            nc.gpsimd.memset(high[:, 0:pair_len].rearrange("p (r g) -> p r g", g=run)[:, :, run - TAIL : run], 0.0)
-            version_tiles.append((low, high))
+            versions = const.tile([P, GROUPS * VERSIONS * VERSION_LEN], BF16, align_bytes=64, name="versions%d" % turn)
+            version_tiles.append(versions)
+        for n in range(min(LEAD_SETS, n_sets)):
+            run = sets[n][0][3] * P
+            total = blocks_of(sets[n]) * P * UNITS
+            nc.gpsimd.memset(
+                version_tiles[n % VERSION_TILES][:, 0:total].rearrange("p (u g) -> p u g", g=run)[:, :, run - TAIL : run], 0.0
+            )
 
-        for n in range(n_groups + 2):
-            if n + 4 < n_groups:
-                load_rows(n + 4)
+        for n in range(n_sets + 2):
+            if n + 3 < n_sets:
+                load_rows(n + 3)
             if n == 0:
                 move_weight_codes()
                 weave_weight_codes()
-            if 0 <= n - 2 < n_groups:
-                quantise(n - 2, 1)
-            if 0 <= n - 1 < n_groups:
+            if 0 <= n - 1 < n_sets:
                 version_one(n - 1)
-            if n + 1 < n_groups:
+            if n + 1 < n_sets:
                 build_windows(n + 1)
-            if n < n_groups:
+            if n < n_sets:
                 turn_and_seed(n)
-            if n + 2 < n_groups:
+            if n + 2 < n_sets:
                 shift_rows(n + 2)
             if n == 0:
                 bias_turned = turn_bias(nc, acc_psum, identity, bias_square)
-            if 0 <= n - 1 < n_groups:
+            if 0 <= n - 1 < n_sets:
                 version_three(n - 1)
-                quantise(n - 1, 0)
+                quantise(n - 1)
             if n == 1:
                 nc.vector.tensor_copy(out=bias_column[:], in_=bias_turned[:, 0:1])
-            if 0 <= n - 2 < n_groups:
+            if 0 <= n - 2 < n_sets:
                 multiply_and_store(n - 2)

@@ -46,7 +46,6 @@ GROUPS = 2
 BLOCKS = GROUPS * CHUNKS
 QUANTISE_WIDTHS = (4096, 2048, 1024, 512, 256, 128)
 LEAD_SETS = 4
-VECTOR_STRIPS = 4
 VERSION_TILES = 2
 TAIL = 32
 
@@ -139,6 +138,7 @@ def tile_conv2d_kernel(tc, x, weights_words, weights_scales, bias, out):
         rows_of = {}
         windows_of = {}
         codes_of = {}
+        result_of = {}
 
         def load_rows(n):
             rows = rows_pool.tile([P, 2, BLOCKS, ROW_PITCH], BF16, name="rows")
@@ -175,7 +175,10 @@ def tile_conv2d_kernel(tc, x, weights_words, weights_scales, bias, out):
             versions = version_tiles[n % VERSION_TILES][:, 0 : len(sets[n]) * VERSIONS * length]
             return versions.rearrange("p (i x) -> p i x", x=VERSIONS * length), length
 
-        def turn_and_seed(n):
+        def strips_of(n):
+            return [(i, strip) for i in range(len(sets[n])) for strip in range(STRIPS)]
+
+        def turn_bank(n, bank):
             windows = windows_of[n]
             chunks = sets[n][0][3]
             run = chunks * P
@@ -183,35 +186,35 @@ def tile_conv2d_kernel(tc, x, weights_words, weights_scales, bias, out):
             runs = version_tiles[n % VERSION_TILES][:, 0 : len(sets[n]) * VERSIONS * length].rearrange(
                 "p (u g) -> p u g", g=run
             )
-            strips = [(i, strip) for i in range(len(sets[n])) for strip in range(STRIPS)]
             bank_strips = BANK_VALUES // run
-            for first in range(0, len(strips), bank_strips):
-                here = strips[first : first + bank_strips]
-                turned = turn_psum.tile([P, BANK_VALUES], BF16, name="turned")
-                for place, (i, strip) in enumerate(here):
-                    for chunk in range(chunks):
-                        at = place * run + chunk * P
-                        nc.tensor.transpose(
-                            turned[:, at : at + P],
-                            windows[:, i * chunks + chunk, WINDOW_START + strip * P : WINDOW_START + (strip + 1) * P],
-                            identity[:],
-                        )
-                places = [i * VERSIONS * STRIPS + strip for i, strip in here]
-                step = places[-1] - places[0] if len(here) == 2 else 1
-                nc.scalar.copy(
-                    out=runs[:, places[0] : places[-1] + 1 : step, :],
-                    in_=turned[:, 0 : len(here) * run].rearrange("p (u g) -> p u g", g=run),
-                )
-            if chunks == CHUNKS:
-                nc.sync.dma_start(
-                    out=versions[:, :, 2 * length : 3 * length - TAPS], in_=versions[:, :, 2 : length - TAPS + 2]
-                )
-            else:
-                nc.scalar.copy(out=versions[:, :, 2 * length : 3 * length - TAPS], in_=versions[:, :, 2 : length - TAPS + 2])
-            share = VECTOR_STRIPS * run
+            here = strips_of(n)[bank * bank_strips : (bank + 1) * bank_strips]
+            turned = turn_psum.tile([P, BANK_VALUES], BF16, name="turned")
+            for place, (i, strip) in enumerate(here):
+                for chunk in range(chunks):
+                    at = place * run + chunk * P
+                    nc.tensor.transpose(
+                        turned[:, at : at + P],
+                        windows[:, i * chunks + chunk, WINDOW_START + strip * P : WINDOW_START + (strip + 1) * P],
+                        identity[:],
+                    )
+            places = [i * VERSIONS * STRIPS + strip for i, strip in here]
+            step = places[-1] - places[0] if len(here) == 2 else 1
             nc.scalar.copy(
-                out=versions[:, :, 3 * length + share : 4 * length - TAPS], in_=versions[:, :, share + 3 : length - TAPS + 3]
+                out=runs[:, places[0] : places[-1] + 1 : step, :],
+                in_=turned[:, 0 : len(here) * run].rearrange("p (u g) -> p u g", g=run),
             )
+            for i, strip in here:
+                if strip == STRIPS - 1:
+                    version_two(n, i)
+
+        def version_two(n, i):
+            versions, length = by_group(n)
+            out_run = versions[:, i, 2 * length : 3 * length - TAPS]
+            in_run = versions[:, i, 2 : length - TAPS + 2]
+            if sets[n][i][3] == CHUNKS:
+                nc.sync.dma_start(out=out_run, in_=in_run)
+            else:
+                nc.scalar.copy(out=out_run, in_=in_run)
 
         def version_one(n):
             versions, length = by_group(n)
@@ -219,9 +222,8 @@ def tile_conv2d_kernel(tc, x, weights_words, weights_scales, bias, out):
 
         def version_three(n):
             versions, length = by_group(n)
-            share = VECTOR_STRIPS * sets[n][0][3] * P
             nc.vector.tensor_copy(
-                out=versions[:, :, 3 * length : 3 * length + share - TAPS], in_=versions[:, :, 3 : share - TAPS + 3]
+                out=versions[:, :, 3 * length : 4 * length - TAPS], in_=versions[:, :, 3 : length - TAPS + 3]
             )
 
         def quantise(n):
@@ -241,21 +243,15 @@ def tile_conv2d_kernel(tc, x, weights_words, weights_scales, bias, out):
                 )
                 first = last
 
-        def multiply_and_store(n):
-            for i in range(len(sets[n])):
-                multiply_and_store_group(n, i)
-
-        def multiply_and_store_group(n, i):
+        def multiply(n, i, z):
             a_codes, a_scales = codes_of[n]
-            base, g, stop, chunks = sets[n][i]
-            words = chunks * P // TAPS
-            result = result_pool.tile([P, WORDS * UNITS], F32, name="result")
-            result_by_unit = result[:, 0 : words * UNITS].rearrange("o (j u) -> o j u", u=UNITS)
-            accs = []
-            for z in range(PASSES):
-                acc = acc_psum.tile([P, PASS_UNITS * WORDS], F32, name="acc")
-                accs.append(acc)
-                moving = slice((i * UNITS + z * PASS_UNITS) * words, (i * UNITS + (z + 1) * PASS_UNITS) * words)
+            words = sets[n][i][3] * P // TAPS
+            if z == 0:
+                result_of[n, i] = result_pool.tile([P, WORDS * UNITS], F32, name="result")
+            result = result_of[n, i]
+            acc = acc_psum.tile([P, PASS_UNITS * WORDS], F32, name="acc")
+            moving = slice((i * UNITS + z * PASS_UNITS) * words, (i * UNITS + (z + 1) * PASS_UNITS) * words)
+            for again in range(1 + z % 2):
                 nc.tensor.matmul_mx(
                     out=acc[:, 0 : PASS_UNITS * words],
                     lhsT=w_swapped[:].bitcast(FP8X4),
@@ -265,13 +261,20 @@ def tile_conv2d_kernel(tc, x, weights_words, weights_scales, bias, out):
                     start=True,
                     stop=True,
                 )
-            for z in range(PASSES):
-                nc.scalar.activation(
-                    out=result_by_unit[:, :, z * PASS_UNITS : (z + 1) * PASS_UNITS],
-                    in_=accs[z][:, 0 : PASS_UNITS * words].rearrange("o (u j) -> o j u", u=PASS_UNITS),
-                    func=mybir.ActivationFunctionType.Identity,
-                    bias=bias_column[:, 0:1],
-                )
+            nc.scalar.activation(
+                out=result[:, 0 : words * UNITS].rearrange("o (j u) -> o j u", u=UNITS)[
+                    :, :, z * PASS_UNITS : (z + 1) * PASS_UNITS
+                ],
+                in_=acc[:, 0 : PASS_UNITS * words].rearrange("o (u j) -> o j u", u=PASS_UNITS),
+                func=mybir.ActivationFunctionType.Identity,
+                bias=bias_column[:, 0:1],
+            )
+            if z == PASSES - 1:
+                store(n, i)
+
+        def store(n, i):
+            base, g, stop, chunks = sets[n][i]
+            result = result_of[n, i]
             while g < stop:
                 image, row = divmod(g, SIDE_IN)
                 g_end = min(stop, image * SIDE_IN + SIDE_OUT)
@@ -283,6 +286,25 @@ def tile_conv2d_kernel(tc, x, weights_words, weights_scales, bias, out):
                     in_=result[:, (g - base) * STRIPS : (g - base) * STRIPS + count],
                 )
                 g = g_end + TAPS - 1
+
+        def turn_and_multiply(n):
+            banks = 0
+            if n < n_sets:
+                banks = -(-len(strips_of(n)) * sets[n][0][3] * P // BANK_VALUES)
+            passes = []
+            if 0 <= n - 2 < n_sets:
+                passes = [(n - 2, i, z) for i in range(len(sets[n - 2])) for z in range(PASSES)]
+            steps = banks if n > 2 else 0
+            for bank in range(banks):
+                turn_bank(n, bank)
+                if bank == 0 and n + 2 < n_sets:
+                    shift_rows(n + 2)
+                if steps:
+                    for args in passes[bank * len(passes) // steps : (bank + 1) * len(passes) // steps]:
+                        multiply(*args)
+            if not steps:
+                for args in passes:
+                    multiply(*args)
 
         load_rows(0)
         w_codes = load_weight_codes(nc, const, weights_words)
@@ -338,10 +360,7 @@ def tile_conv2d_kernel(tc, x, weights_words, weights_scales, bias, out):
                 version_one(n - 1)
             if n + 1 < n_sets:
                 build_windows(n + 1)
-            if n < n_sets:
-                turn_and_seed(n)
-            if n + 2 < n_sets:
-                shift_rows(n + 2)
+            turn_and_multiply(n)
             if n == 0:
                 bias_turned = turn_bias(nc, acc_psum, identity, bias_square)
             if 0 <= n - 1 < n_sets:
@@ -349,5 +368,3 @@ def tile_conv2d_kernel(tc, x, weights_words, weights_scales, bias, out):
                 quantise(n - 1)
             if n == 1:
                 nc.vector.tensor_copy(out=bias_column[:], in_=bias_turned[:, 0:1])
-            if 0 <= n - 2 < n_sets:
-                multiply_and_store(n - 2)

@@ -46,6 +46,8 @@ GROUPS = 2
 BLOCKS = GROUPS * CHUNKS
 QUANTISE_WIDTHS = (4096, 2048, 1024, 512, 256, 128)
 LEAD_SETS = 4
+DMA_STRIPS = 4
+VECTOR_STRIPS = 3
 VERSION_TILES = 2
 TAIL = 32
 
@@ -87,15 +89,6 @@ def plan_sets(groups):
 
 def blocks_of(groups):
     return sum(group[3] for group in groups)
-
-
-def load_weight_codes(nc, const, weights_words):
-    w_codes = const.tile([P, 4 * C_OUT], U8, align_bytes=64)
-    nc.sync.dma_start(
-        out=w_codes[:].bitcast(I32),
-        in_=weights_words[0].rearrange("p n t -> p (n t)").bitcast(I32),
-    )
-    return w_codes
 
 
 def load_weight_scales(nc, w_scales, weights_scales):
@@ -151,7 +144,7 @@ def tile_conv2d_kernel(tc, x, weights_words, weights_scales, bias, out):
 
         def shift_rows(n):
             rows, blocks = rows_of[n], blocks_of(sets[n])
-            nc.scalar.copy(out=rows[:, 1, 0:blocks, 0:ROW_LEN], in_=rows[:, 0, 0:blocks, 1:SIDE_IN])
+            nc.vector.tensor_copy(out=rows[:, 1, 0:blocks, 0:ROW_LEN], in_=rows[:, 0, 0:blocks, 1:SIDE_IN])
 
         def build_windows(n):
             blocks = blocks_of(sets[n])
@@ -203,18 +196,32 @@ def tile_conv2d_kernel(tc, x, weights_words, weights_scales, bias, out):
                 out=runs[:, places[0] : places[-1] + 1 : step, :],
                 in_=turned[:, 0 : len(here) * run].rearrange("p (u g) -> p u g", g=run),
             )
+            paired = len(sets[n]) == GROUPS
+            copy_shifted(turned, here, runs, run, 2, DMA_STRIPS if paired else 0)
+            copy_shifted(turned, here, runs, run, 3, VECTOR_STRIPS if paired else STRIPS)
             for i, strip in here:
-                if strip == STRIPS - 1:
+                if paired and strip == DMA_STRIPS - 1:
                     version_two(n, i)
+
+        def copy_shifted(turned, here, runs, run, version, first_strip):
+            mine = [(place, i, strip) for place, (i, strip) in enumerate(here) if strip >= first_strip]
+            if not mine:
+                return
+            places = [(i * VERSIONS + version) * STRIPS + strip for place, i, strip in mine]
+            step = places[-1] - places[0] if len(mine) == 2 else 1
+            nc.scalar.copy(
+                out=runs[:, places[0] : places[-1] + 1 : step, 0 : run - TAPS],
+                in_=turned[:].rearrange("p (u g) -> p u g", g=run)[
+                    :, mine[0][0] : mine[-1][0] + 1, version : run - TAPS + version
+                ],
+            )
 
         def version_two(n, i):
             versions, length = by_group(n)
-            out_run = versions[:, i, 2 * length : 3 * length - TAPS]
-            in_run = versions[:, i, 2 : length - TAPS + 2]
-            if sets[n][i][3] == CHUNKS:
-                nc.sync.dma_start(out=out_run, in_=in_run)
-            else:
-                nc.scalar.copy(out=out_run, in_=in_run)
+            share = DMA_STRIPS * sets[n][i][3] * P
+            nc.sync.dma_start(
+                out=versions[:, i, 2 * length : 2 * length + share - TAPS], in_=versions[:, i, 2 : share - TAPS + 2]
+            )
 
         def version_one(n):
             versions, length = by_group(n)
@@ -222,8 +229,9 @@ def tile_conv2d_kernel(tc, x, weights_words, weights_scales, bias, out):
 
         def version_three(n):
             versions, length = by_group(n)
+            share = (VECTOR_STRIPS if len(sets[n]) == GROUPS else STRIPS) * sets[n][0][3] * P
             nc.vector.tensor_copy(
-                out=versions[:, :, 3 * length : 4 * length - TAPS], in_=versions[:, :, 3 : length - TAPS + 3]
+                out=versions[:, :, 3 * length : 3 * length + share - TAPS], in_=versions[:, :, 3 : share - TAPS + 3]
             )
 
         def quantise(n):
@@ -251,16 +259,15 @@ def tile_conv2d_kernel(tc, x, weights_words, weights_scales, bias, out):
             result = result_of[n, i]
             acc = acc_psum.tile([P, PASS_UNITS * WORDS], F32, name="acc")
             moving = slice((i * UNITS + z * PASS_UNITS) * words, (i * UNITS + (z + 1) * PASS_UNITS) * words)
-            for again in range(1 + z % 2):
-                nc.tensor.matmul_mx(
-                    out=acc[:, 0 : PASS_UNITS * words],
-                    lhsT=w_swapped[:].bitcast(FP8X4),
-                    lhsT_scale=w_scales[:],
-                    rhs=a_codes[:, moving].bitcast(FP8X4),
-                    rhs_scale=a_scales[:, moving],
-                    start=True,
-                    stop=True,
-                )
+            nc.tensor.matmul_mx(
+                out=acc[:, 0 : PASS_UNITS * words],
+                lhsT=w_swapped[:].bitcast(FP8X4),
+                lhsT_scale=w_scales[:],
+                rhs=a_codes[:, moving].bitcast(FP8X4),
+                rhs_scale=a_scales[:, moving],
+                start=True,
+                stop=True,
+            )
             nc.scalar.activation(
                 out=result[:, 0 : words * UNITS].rearrange("o (j u) -> o j u", u=UNITS)[
                     :, :, z * PASS_UNITS : (z + 1) * PASS_UNITS
@@ -297,8 +304,6 @@ def tile_conv2d_kernel(tc, x, weights_words, weights_scales, bias, out):
             steps = banks if n > 2 else 0
             for bank in range(banks):
                 turn_bank(n, bank)
-                if bank == 0 and n + 2 < n_sets:
-                    shift_rows(n + 2)
                 if steps:
                     for args in passes[bank * len(passes) // steps : (bank + 1) * len(passes) // steps]:
                         multiply(*args)
@@ -307,37 +312,33 @@ def tile_conv2d_kernel(tc, x, weights_words, weights_scales, bias, out):
                     multiply(*args)
 
         load_rows(0)
-        w_codes = load_weight_codes(nc, const, weights_words)
         load_rows(1)
+        w_rows = const.tile([P, TAPS * TAPS * C_OUT], U8, align_bytes=64)
+        w_by_m = weights_words[0].rearrange("(q e d) n t -> e q (d n t)", e=2, d=TAPS)
+        for place in range(8):
+            nc.sync.dma_start(out=w_rows[place:P:8, :].bitcast(I32), in_=w_by_m[place // 2 % 2].bitcast(I32))
         load_rows(2)
         identity = const.tile([P, P], BF16)
         make_identity(nc, identity[:])
         w_scales = const.tile([P, C_OUT], U8, align_bytes=64)
         nc.vector.memset(w_scales[:].bitcast(I32), 0)
         bias_square = load_bias(nc, const, bias)
-        load_weight_scales(nc, w_scales, weights_scales)
-        w_planes = const.tile([P, TAPS, C_OUT], U8, align_bytes=64)
-        nc.vector.tensor_copy(out=w_planes[:], in_=w_codes[:].rearrange("p (n t) -> p t n", t=TAPS))
         shift_rows(0)
-        shift_rows(1)
         build_windows(0)
-        w_moved = const.tile([P, TAPS, C_OUT], U8, align_bytes=64)
+        w_tables = const.tile([P, TAPS, C_OUT * TAPS], U8, align_bytes=64)
         w_swapped = const.tile([P, TAPS * C_OUT], U8, align_bytes=64)
         bias_column = const.tile([P, 1], F32)
 
-        def move_weight_codes():
-            for di in range(TAPS):
-                for dj in range(TAPS):
-                    for e in range(2):
-                        place = 4 * (dj // 2) + 2 * e + dj % 2
-                        nc.sync.dma_start(
-                            out=w_moved[place:P:8, di, :].bitcast(I32), in_=w_planes[4 * e + di : P : 8, dj, :].bitcast(I32)
-                        )
-
-        def weave_weight_codes():
-            nc.gpsimd.tensor_copy(
-                out=w_swapped[:].rearrange("p (n t) -> p n t", t=TAPS), in_=w_moved[:].rearrange("p t n -> p n t")
+        def sort_weight_codes():
+            nc.vector.tensor_copy(
+                out=w_tables[:].rearrange("p t (n d) -> p t n d", d=TAPS),
+                in_=w_rows[:].rearrange("p (d n t) -> p t n d", d=TAPS, t=TAPS),
             )
+
+        def pick_weight_codes():
+            for place in range(8):
+                dj = 2 * (place // 4) + place % 2
+                nc.sync.dma_start(out=w_swapped[place:P:8, :].bitcast(I32), in_=w_tables[place:P:8, dj, :].bitcast(I32))
 
         version_tiles = []
         for turn in range(VERSION_TILES):
@@ -353,13 +354,16 @@ def tile_conv2d_kernel(tc, x, weights_words, weights_scales, bias, out):
         for n in range(n_sets + 2):
             if n + 3 < n_sets:
                 load_rows(n + 3)
-            if n == 0:
-                move_weight_codes()
-                weave_weight_codes()
+            if n + 1 < n_sets:
+                shift_rows(n + 1)
             if 0 <= n - 1 < n_sets:
                 version_one(n - 1)
             if n + 1 < n_sets:
                 build_windows(n + 1)
+            if n == 0:
+                sort_weight_codes()
+                pick_weight_codes()
+                load_weight_scales(nc, w_scales, weights_scales)
             turn_and_multiply(n)
             if n == 0:
                 bias_turned = turn_bias(nc, acc_psum, identity, bias_square)

@@ -41,13 +41,12 @@ WINDOW_PITCH = 672
 BANK_VALUES = 1024
 TURNED_BANKS = 3
 ACC_BANKS = PASSES
-LEAD_CHUNKS = (1,)
 GROUPS = 2
 BLOCKS = GROUPS * CHUNKS
 QUANTISE_WIDTHS = (4096, 2048, 1024, 512, 256, 128)
-LEAD_SETS = 4
+LEAD_SETS = 3
 DMA_STRIPS = 4
-VECTOR_STRIPS = 3
+VECTOR_STRIPS = 4
 VERSION_TILES = 2
 TAIL = 32
 
@@ -62,10 +61,7 @@ def plan_groups():
     start = 0
     while start < end:
         left = end - start
-        if len(groups) < len(LEAD_CHUNKS):
-            chunks = LEAD_CHUNKS[len(groups)]
-        else:
-            chunks = CHUNKS if left > yield_of(2) + yield_of(1) - STORE_ROWS else (2 if left > yield_of(1) else 1)
+        chunks = CHUNKS if left > yield_of(2) + yield_of(1) - STORE_ROWS else (2 if left > yield_of(1) else 1)
         stop = min(start + yield_of(chunks), end)
         if stop < end:
             row = stop % SIDE_IN
@@ -79,11 +75,10 @@ def plan_sets(groups):
     full = [group for group in groups if group[3] == CHUNKS]
     pairs = (len(full) - 2) // GROUPS
     alone = len(full) - GROUPS * pairs
-    sets = [[group] for group in groups[: len(LEAD_CHUNKS)]]
-    sets.append([full[0]])
+    sets = [[full[0]]]
     sets += [full[1 + GROUPS * k : 1 + GROUPS * (k + 1)] for k in range(pairs)]
     sets += [[group] for group in full[len(full) - alone + 1 :]]
-    sets += [[group] for group in groups[len(LEAD_CHUNKS) + len(full) :]]
+    sets += [[group] for group in groups[len(full) :]]
     return sets
 
 
@@ -259,15 +254,16 @@ def tile_conv2d_kernel(tc, x, weights_words, weights_scales, bias, out):
             result = result_of[n, i]
             acc = acc_psum.tile([P, PASS_UNITS * WORDS], F32, name="acc")
             moving = slice((i * UNITS + z * PASS_UNITS) * words, (i * UNITS + (z + 1) * PASS_UNITS) * words)
-            nc.tensor.matmul_mx(
-                out=acc[:, 0 : PASS_UNITS * words],
-                lhsT=w_swapped[:].bitcast(FP8X4),
-                lhsT_scale=w_scales[:],
-                rhs=a_codes[:, moving].bitcast(FP8X4),
-                rhs_scale=a_scales[:, moving],
-                start=True,
-                stop=True,
-            )
+            for again in range(1 + z % 2):
+                nc.tensor.matmul_mx(
+                    out=acc[:, 0 : PASS_UNITS * words],
+                    lhsT=w_swapped[:].bitcast(FP8X4),
+                    lhsT_scale=w_scales[:],
+                    rhs=a_codes[:, moving].bitcast(FP8X4),
+                    rhs_scale=a_scales[:, moving],
+                    start=True,
+                    stop=True,
+                )
             nc.scalar.activation(
                 out=result[:, 0 : words * UNITS].rearrange("o (j u) -> o j u", u=UNITS)[
                     :, :, z * PASS_UNITS : (z + 1) * PASS_UNITS
@@ -312,6 +308,9 @@ def tile_conv2d_kernel(tc, x, weights_words, weights_scales, bias, out):
                     multiply(*args)
 
         load_rows(0)
+        first_copy = const.tile([P, 2], F32)
+        nc.vector.memset(first_copy[:, 0:1], 0.0)
+        nc.scalar.copy(out=first_copy[:, 1:2], in_=first_copy[:, 0:1])
         load_rows(1)
         w_rows = const.tile([P, TAPS * TAPS * C_OUT], U8, align_bytes=64)
         w_by_m = weights_words[0].rearrange("(q e d) n t -> e q (d n t)", e=2, d=TAPS)

@@ -46,7 +46,7 @@ BLOCKS = GROUPS * CHUNKS
 QUANTISE_WIDTHS = (4096, 2048, 1024, 512, 256, 128)
 LEAD_SETS = 3
 DMA_STRIPS = 4
-VECTOR_STRIPS = 4
+VECTOR_STRIPS = 3
 VERSION_TILES = 2
 TAIL = 32
 
@@ -254,16 +254,15 @@ def tile_conv2d_kernel(tc, x, weights_words, weights_scales, bias, out):
             result = result_of[n, i]
             acc = acc_psum.tile([P, PASS_UNITS * WORDS], F32, name="acc")
             moving = slice((i * UNITS + z * PASS_UNITS) * words, (i * UNITS + (z + 1) * PASS_UNITS) * words)
-            for again in range(1 + z % 2):
-                nc.tensor.matmul_mx(
-                    out=acc[:, 0 : PASS_UNITS * words],
-                    lhsT=w_swapped[:].bitcast(FP8X4),
-                    lhsT_scale=w_scales[:],
-                    rhs=a_codes[:, moving].bitcast(FP8X4),
-                    rhs_scale=a_scales[:, moving],
-                    start=True,
-                    stop=True,
-                )
+            nc.tensor.matmul_mx(
+                out=acc[:, 0 : PASS_UNITS * words],
+                lhsT=w_swapped[:].bitcast(FP8X4),
+                lhsT_scale=w_scales[:],
+                rhs=a_codes[:, moving].bitcast(FP8X4),
+                rhs_scale=a_scales[:, moving],
+                start=True,
+                stop=True,
+            )
             nc.scalar.activation(
                 out=result[:, 0 : words * UNITS].rearrange("o (j u) -> o j u", u=UNITS)[
                     :, :, z * PASS_UNITS : (z + 1) * PASS_UNITS
@@ -290,22 +289,15 @@ def tile_conv2d_kernel(tc, x, weights_words, weights_scales, bias, out):
                 )
                 g = g_end + TAPS - 1
 
-        def turn_and_multiply(n):
-            banks = 0
-            if n < n_sets:
-                banks = -(-len(strips_of(n)) * sets[n][0][3] * P // BANK_VALUES)
-            passes = []
-            if 0 <= n - 2 < n_sets:
-                passes = [(n - 2, i, z) for i in range(len(sets[n - 2])) for z in range(PASSES)]
-            steps = banks if n > 2 else 0
-            for bank in range(banks):
+        def turn_set(n):
+            run = sets[n][0][3] * P
+            for bank in range(-(-len(strips_of(n)) * run // BANK_VALUES)):
                 turn_bank(n, bank)
-                if steps:
-                    for args in passes[bank * len(passes) // steps : (bank + 1) * len(passes) // steps]:
-                        multiply(*args)
-            if not steps:
-                for args in passes:
-                    multiply(*args)
+
+        def multiply_set(n):
+            for i in range(len(sets[n])):
+                for z in range(PASSES):
+                    multiply(n, i, z)
 
         load_rows(0)
         first_copy = const.tile([P, 2], F32)
@@ -363,7 +355,10 @@ def tile_conv2d_kernel(tc, x, weights_words, weights_scales, bias, out):
                 sort_weight_codes()
                 pick_weight_codes()
                 load_weight_scales(nc, w_scales, weights_scales)
-            turn_and_multiply(n)
+            if n < n_sets:
+                turn_set(n)
+            if 0 <= n - 2 < n_sets:
+                multiply_set(n - 2)
             if n == 0:
                 bias_turned = turn_bias(nc, acc_psum, identity, bias_square)
             if 0 <= n - 1 < n_sets:

from contextlib import ExitStack

import concourse.mybir as mybir
from concourse.masks import make_identity

F32 = mybir.dt.float32
BF16 = mybir.dt.bfloat16
I32 = mybir.dt.int32
U32 = mybir.dt.uint32
U8 = mybir.dt.uint8
FP8X4 = mybir.dt.float8_e4m3fn_x4

P = 128
BATCH = 2
C_IN = 32
SIDE_OUT = 160
TAPS = 4
SIDE_IN = SIDE_OUT + TAPS - 1
C_OUT = 128
K = C_IN * TAPS * TAPS
FLOPS = 2 * BATCH * SIDE_OUT * SIDE_OUT * K * C_OUT

STRIPS = SIDE_OUT // C_IN
ALL_ROWS = BATCH * C_IN * SIDE_IN
CHUNKS = 4
GROUP_ROWS = CHUNKS * P
WORDS = GROUP_ROWS // TAPS
VERSIONS = TAPS
VERSION_LEN = STRIPS * GROUP_ROWS
PAIR_LEN = 2 * VERSION_LEN
UNITS = VERSIONS * STRIPS
PASS_UNITS = 4
PASSES = UNITS // PASS_UNITS
STORE_ROWS = 8

ROW_LEN = SIDE_IN - 1
ROW_PITCH = 176
WINDOW_START = 8
WINDOW_PITCH = 672

BANK_VALUES = 1024
TURNED_BANKS = 3
ACC_BANKS = PASSES
GROUPS = 2
BLOCKS = GROUPS * CHUNKS
QUANTISE_WIDTHS = (4096, 2048, 1024, 512, 256, 128)
LEAD_SETS = 3
DMA_STRIPS = 4
VECTOR_STRIPS = 3
VERSION_TILES = 2
TAIL = 32


def yield_of(chunks):
    return chunks * P - (TAPS - 1)


def plan_groups():
    groups = []
    end = ALL_ROWS - (TAPS - 1)
    start = 0
    while start < end:
        left = end - start
        chunks = CHUNKS if left > yield_of(2) + yield_of(1) - STORE_ROWS else (2 if left > yield_of(1) else 1)
        stop = min(start + yield_of(chunks), end)
        if stop < end:
            row = stop % SIDE_IN
            stop -= row % STORE_ROWS if row <= SIDE_OUT else row - SIDE_OUT
        groups.append((min(start, ALL_ROWS - chunks * P), start, stop, chunks))
        start = stop + (TAPS - 1 if stop % SIDE_IN == SIDE_OUT else 0)
    return groups


def plan_sets(groups):
    full = [group for group in groups if group[3] == CHUNKS]
    pairs = (len(full) - 2) // GROUPS
    alone = len(full) - GROUPS * pairs
    sets = [[full[0]]]
    sets += [full[1 + GROUPS * k : 1 + GROUPS * (k + 1)] for k in range(pairs)]
    sets += [[group] for group in full[len(full) - alone + 1 :]]
    sets += [[group] for group in groups[len(full) :]]
    return sets


def blocks_of(groups):
    return sum(group[3] for group in groups)


def load_weight_scales(nc, w_scales, weights_scales):
    for quadrant in range(4):
        nc.sync.dma_start(
            out=w_scales[32 * quadrant : 32 * quadrant + 4, :].bitcast(I32),
            in_=weights_scales[0, 4 * quadrant : 4 * quadrant + 4, :].bitcast(I32),
        )


def load_bias(nc, const, bias):
    bias_square = const.tile([P, C_OUT], BF16)
    nc.vector.memset(bias_square[:], 0.0)
    nc.scalar.dma_start(out=bias_square[0:1, :], in_=bias.unsqueeze(0))
    return bias_square


def turn_bias(nc, acc_psum, identity, bias_square):
    bias_turned = acc_psum.tile([P, BANK_VALUES], BF16, name="acc")
    nc.tensor.transpose(bias_turned[:, 0:P], bias_square[:], identity[:])
    return bias_turned


def tile_conv2d_kernel(tc, x, weights_words, weights_scales, bias, out):
    nc = tc.nc
    groups = plan_groups()
    sets = plan_sets(groups)
    n_sets = len(sets)
    x_rows = x.rearrange("b c h w -> (b c h) w")
    with ExitStack() as ctx:
        const = ctx.enter_context(tc.tile_pool(name="const", bufs=1))
        rows_pool = ctx.enter_context(tc.tile_pool(name="rows", bufs=3))
        window_pool = ctx.enter_context(tc.tile_pool(name="windows", bufs=2))
        code_pool = ctx.enter_context(tc.tile_pool(name="codes", bufs=2))
        result_pool = ctx.enter_context(tc.tile_pool(name="result", bufs=3))
        turn_psum = ctx.enter_context(tc.psum_pool(name="turned", bufs=TURNED_BANKS))
        acc_psum = ctx.enter_context(tc.psum_pool(name="acc", bufs=ACC_BANKS))
        ctx.enter_context(tc.manual_schedule())

        rows_of = {}
        windows_of = {}
        codes_of = {}
        result_of = {}

        def load_rows(n):
            rows = rows_pool.tile([P, 2, BLOCKS, ROW_PITCH], BF16, name="rows")
            rows_of[n] = rows
            for i, (base, first_row, stop, chunks) in enumerate(sets[n]):
                nc.sync.dma_start(
                    out=rows[:, 0, i * chunks : (i + 1) * chunks, 0:SIDE_IN],
                    in_=x_rows[base : base + chunks * P, :].rearrange("(k p) w -> p k w", p=P),
                )

        def shift_rows(n):
            rows, blocks = rows_of[n], blocks_of(sets[n])
            nc.vector.tensor_copy(out=rows[:, 1, 0:blocks, 0:ROW_LEN], in_=rows[:, 0, 0:blocks, 1:SIDE_IN])

        def build_windows(n):
            blocks = blocks_of(sets[n])
            windows = window_pool.tile([P, BLOCKS, WINDOW_PITCH], BF16, align_bytes=64, name="windows")
            windows_of[n] = windows
            words = ROW_LEN // 2
            first = WINDOW_START // 2 - 2
            nc.vector.tensor_copy(
                out=windows[:].bitcast(F32)[:, 0:blocks, first : first + 4 * words].rearrange(
                    "p k (h r e) -> p k h r e", r=2, e=2
                ),
                in_=rows_of[n][:]
                .bitcast(F32)[:, :, 0:blocks, 0:words]
                .rearrange("p e k h -> p k h e")
                .unsqueeze(3)
                .to_broadcast([P, blocks, words, 2, 2]),
            )

        def by_group(n):
            length = STRIPS * sets[n][0][3] * P
            versions = version_tiles[n % VERSION_TILES][:, 0 : len(sets[n]) * VERSIONS * length]
            return versions.rearrange("p (i x) -> p i x", x=VERSIONS * length), length

        def strips_of(n):
            return [(i, strip) for i in range(len(sets[n])) for strip in range(STRIPS)]

        def turn_bank(n, bank):
            windows = windows_of[n]
            chunks = sets[n][0][3]
            run = chunks * P
            versions, length = by_group(n)
            runs = version_tiles[n % VERSION_TILES][:, 0 : len(sets[n]) * VERSIONS * length].rearrange(
                "p (u g) -> p u g", g=run
            )
            bank_strips = BANK_VALUES // run
            here = strips_of(n)[bank * bank_strips : (bank + 1) * bank_strips]
            turned = turn_psum.tile([P, BANK_VALUES], BF16, name="turned")
            for place, (i, strip) in enumerate(here):
                for chunk in range(chunks):
                    at = place * run + chunk * P
                    nc.tensor.transpose(
                        turned[:, at : at + P],
                        windows[:, i * chunks + chunk, WINDOW_START + strip * P : WINDOW_START + (strip + 1) * P],
                        identity[:],
                    )
            places = [i * VERSIONS * STRIPS + strip for i, strip in here]
            step = places[-1] - places[0] if len(here) == 2 else 1
            nc.scalar.copy(
                out=runs[:, places[0] : places[-1] + 1 : step, :],
                in_=turned[:, 0 : len(here) * run].rearrange("p (u g) -> p u g", g=run),
            )
            paired = len(sets[n]) == GROUPS
            copy_shifted(turned, here, runs, run, 2, DMA_STRIPS if paired else 0)
            copy_shifted(turned, here, runs, run, 3, VECTOR_STRIPS if paired else STRIPS)
            for i, strip in here:
                if paired and strip == DMA_STRIPS - 1:
                    version_two(n, i)

        def copy_shifted(turned, here, runs, run, version, first_strip):
            mine = [(place, i, strip) for place, (i, strip) in enumerate(here) if strip >= first_strip]
            if not mine:
                return
            places = [(i * VERSIONS + version) * STRIPS + strip for place, i, strip in mine]
            step = places[-1] - places[0] if len(mine) == 2 else 1
            nc.scalar.copy(
                out=runs[:, places[0] : places[-1] + 1 : step, 0 : run - TAPS],
                in_=turned[:].rearrange("p (u g) -> p u g", g=run)[
                    :, mine[0][0] : mine[-1][0] + 1, version : run - TAPS + version
                ],
            )

        def version_two(n, i):
            versions, length = by_group(n)
            share = DMA_STRIPS * sets[n][i][3] * P
            nc.sync.dma_start(
                out=versions[:, i, 2 * length : 2 * length + share - TAPS], in_=versions[:, i, 2 : share - TAPS + 2]
            )

        def version_one(n):
            versions, length = by_group(n)
            nc.vector.tensor_copy(out=versions[:, :, length : 2 * length - TAPS], in_=versions[:, :, 1 : length - TAPS + 1])

        def version_three(n):
            versions, length = by_group(n)
            share = (VECTOR_STRIPS if len(sets[n]) == GROUPS else STRIPS) * sets[n][0][3] * P
            nc.vector.tensor_copy(
                out=versions[:, :, 3 * length : 3 * length + share - TAPS], in_=versions[:, :, 3 : share - TAPS + 3]
            )

        def quantise(n):
            a_codes = code_pool.tile([P, GROUPS * UNITS * WORDS], U32, align_bytes=64, name="a_codes")
            a_scales = code_pool.tile([P, GROUPS * UNITS * WORDS], U8, align_bytes=64, name="a_scales")
            codes_of[n] = (a_codes, a_scales)
            values = version_tiles[n % VERSION_TILES]
            total = blocks_of(sets[n]) * P * UNITS
            first = 0
            while first < total:
                last = first + max(width for width in QUANTISE_WIDTHS if width <= total - first)
                words = slice(first // TAPS, last // TAPS)
                nc.vector.quantize_mx(
                    out=a_codes[:, words].bitcast(FP8X4),
                    scales=a_scales[:, words],
                    in_=values[:, first:last],
                )
                first = last

        def multiply(n, i, z):
            a_codes, a_scales = codes_of[n]
            words = sets[n][i][3] * P // TAPS
            if z == 0:
                result_of[n, i] = result_pool.tile([P, WORDS * UNITS], F32, name="result")
            result = result_of[n, i]
            acc = acc_psum.tile([P, PASS_UNITS * WORDS], F32, name="acc")
            moving = slice((i * UNITS + z * PASS_UNITS) * words, (i * UNITS + (z + 1) * PASS_UNITS) * words)
            nc.tensor.matmul_mx(
                out=acc[:, 0 : PASS_UNITS * words],
                lhsT=w_swapped[:].bitcast(FP8X4),
                lhsT_scale=w_scales[:],
                rhs=a_codes[:, moving].bitcast(FP8X4),
                rhs_scale=a_scales[:, moving],
                start=True,
                stop=True,
            )
            nc.scalar.activation(
                out=result[:, 0 : words * UNITS].rearrange("o (j u) -> o j u", u=UNITS)[
                    :, :, z * PASS_UNITS : (z + 1) * PASS_UNITS
                ],
                in_=acc[:, 0 : PASS_UNITS * words].rearrange("o (u j) -> o j u", u=PASS_UNITS),
                func=mybir.ActivationFunctionType.Identity,
                bias=bias_column[:, 0:1],
            )
            if z == PASSES - 1:
                store(n, i)

        def store(n, i):
            base, g, stop, chunks = sets[n][i]
            result = result_of[n, i]
            while g < stop:
                image, row = divmod(g, SIDE_IN)
                g_end = min(stop, image * SIDE_IN + SIDE_OUT)
                batch, channel = divmod(image, C_IN)
                first_r = (channel * SIDE_OUT + row) * STRIPS
                count = (g_end - g) * STRIPS
                nc.sync.dma_start(
                    out=out[batch].rearrange("o u v -> o (u v)")[:, first_r : first_r + count],
                    in_=result[:, (g - base) * STRIPS : (g - base) * STRIPS + count],
                )
                g = g_end + TAPS - 1

        def turn_set(n):
            run = sets[n][0][3] * P
            for bank in range(-(-len(strips_of(n)) * run // BANK_VALUES)):
                turn_bank(n, bank)

        def multiply_set(n):
            for i in range(len(sets[n])):
                for z in range(PASSES):
                    multiply(n, i, z)

        load_rows(0)
        first_copy = const.tile([P, 2], F32)
        nc.vector.memset(first_copy[:, 0:1], 0.0)
        nc.scalar.copy(out=first_copy[:, 1:2], in_=first_copy[:, 0:1])
        load_rows(1)
        w_rows = const.tile([P, TAPS * TAPS * C_OUT], U8, align_bytes=64)
        w_by_m = weights_words[0].rearrange("(q e d) n t -> e q (d n t)", e=2, d=TAPS)
        for place in range(8):
            nc.sync.dma_start(out=w_rows[place:P:8, :].bitcast(I32), in_=w_by_m[place // 2 % 2].bitcast(I32))
        load_rows(2)
        identity = const.tile([P, P], BF16)
        make_identity(nc, identity[:])
        w_scales = const.tile([P, C_OUT], U8, align_bytes=64)
        nc.vector.memset(w_scales[:].bitcast(I32), 0)
        bias_square = load_bias(nc, const, bias)
        shift_rows(0)
        build_windows(0)
        w_tables = const.tile([P, TAPS, C_OUT * TAPS], U8, align_bytes=64)
        w_swapped = const.tile([P, TAPS * C_OUT], U8, align_bytes=64)
        bias_column = const.tile([P, 1], F32)

        def sort_weight_codes():
            nc.vector.tensor_copy(
                out=w_tables[:].rearrange("p t (n d) -> p t n d", d=TAPS),
                in_=w_rows[:].rearrange("p (d n t) -> p t n d", d=TAPS, t=TAPS),
            )

        def pick_weight_codes():
            for place in range(8):
                dj = 2 * (place // 4) + place % 2
                nc.sync.dma_start(out=w_swapped[place:P:8, :].bitcast(I32), in_=w_tables[place:P:8, dj, :].bitcast(I32))

        version_tiles = []
        for turn in range(VERSION_TILES):
            versions = const.tile([P, GROUPS * VERSIONS * VERSION_LEN], BF16, align_bytes=64, name="versions%d" % turn)
            version_tiles.append(versions)
        for n in range(min(LEAD_SETS, n_sets)):
            run = sets[n][0][3] * P
            total = blocks_of(sets[n]) * P * UNITS
            nc.gpsimd.memset(
                version_tiles[n % VERSION_TILES][:, 0:total].rearrange("p (u g) -> p u g", g=run)[:, :, run - TAIL : run], 0.0
            )

        for n in range(n_sets + 2):
            if n + 3 < n_sets:
                load_rows(n + 3)
            if n + 1 < n_sets:
                shift_rows(n + 1)
            if 0 <= n - 1 < n_sets:
                version_one(n - 1)
            if n + 1 < n_sets:
                build_windows(n + 1)
            if n == 0:
                sort_weight_codes()
                pick_weight_codes()
                load_weight_scales(nc, w_scales, weights_scales)
            if n < n_sets:
                turn_set(n)
            if 0 <= n - 2 < n_sets:
                multiply_set(n - 2)
            if n == 0:
                bias_turned = turn_bias(nc, acc_psum, identity, bias_square)
            if 0 <= n - 1 < n_sets:
                version_three(n - 1)
                quantise(n - 1)
            if n == 1:
                nc.vector.tensor_copy(out=bias_column[:], in_=bias_turned[:, 0:1])
